import numpy as np
import ml_dtypes


def mxq(x, axis, fmt="e4m3"):
    dtype, down = {"e4m3": (ml_dtypes.float8_e4m3fn, 7), "e5m2": (ml_dtypes.float8_e5m2, 14)}[fmt]
    v = np.moveaxis(np.asarray(x, np.float32).astype(ml_dtypes.bfloat16).astype(np.float64), axis, -1)
    blocks = v.reshape(v.shape[:-1] + (-1, 32))
    amax = np.abs(blocks).max(-1, keepdims=True)
    byte = np.maximum(np.where(amax > 0, np.frexp(amax)[1] - 1 + 127, 0) - down, 1)
    scale = np.exp2(byte - 127.0)
    codes = (blocks / scale).astype(np.float32).astype(dtype).astype(np.float64)
    return np.moveaxis((codes * scale).reshape(v.shape), -1, axis)


WIDE = False


def mx_kscale(k):
    if not WIDE:
        return np.ones(k)
    levels = np.array([10, -10, 5, -5, 0])
    if k % 512:
        return np.exp2(np.random.permutation(np.resize(levels, k // 32))).repeat(32)
    a = np.empty((k // 512, 16))
    for p in range(k // 512):
        a[p, :8] = np.random.permutation(np.resize(levels, 8))
        for g in range(8):
            far = levels[np.abs(levels - a[p, g]) >= 10]
            a[p, g + 8] = far[np.random.randint(len(far))]
    return np.exp2(a.ravel()).repeat(32)


BF16 = ml_dtypes.bfloat16


def bf(x):
    return np.asarray(x, np.float32).astype(BF16)


def f64(x):
    return np.asarray(x).astype(np.float64)


B, N, E, H, C = 2, 2048, 256, 2, 512
D = E // H


def decay_gammas():
    return 1.0 - np.exp(np.linspace(np.log(2.0 ** -5), np.log(2.0 ** -9), H))


def setup_inputs():
    t = mx_kscale(N)
    return {"q_rot": bf(np.random.standard_normal((B, H, N, D))),
            "k_scaled": bf(np.random.standard_normal((B, H, N, D)) / np.sqrt(D) * t[:, None]),
            "v": bf(np.random.standard_normal((B, H, N, D)) * 0.5 / t[:, None])}


def reference(q_rot, k_scaled, v):
    q, k = f64(q_rot), f64(k_scaled)
    vq = mxq(f64(v), 2, "e4m3")
    gam = decay_gammas()[:, None, None]
    out = []
    for i in range(N // C):
        lo, hi = i * C, (i + 1) * C
        dist = f64(np.arange(lo, hi))[:, None] - f64(np.arange(hi))[None, :]
        mask = gam ** np.where(dist < 0, np.inf, dist)
        sim = (q[:, :, lo:hi] @ k[:, :, :hi].transpose(0, 1, 3, 2)) * mask[None]
        out.append(mxq(sim, 3, "e4m3") @ vq[:, :, :hi])
    ret = np.concatenate(out, axis=2)
    return ret.transpose(0, 2, 1, 3).reshape(B, N, E)

@@ -1,0 +1,231 @@
+import math
+from contextlib import ExitStack
+
+import concourse.mybir as mybir
+from concourse.masks import make_identity
+
+BF16 = mybir.dt.bfloat16
+F32 = mybir.dt.float32
+I32 = mybir.dt.int32
+U32 = mybir.dt.uint32
+U8 = mybir.dt.uint8
+FP8X4 = mybir.dt.float8_e4m3fn_x4
+
+P = 128
+PACK = 4
+CHUNK = P * PACK
+B, H, N, D = 2, 2, 2048, 128
+PAIRS = B * H
+CHUNKS = N // CHUNK
+TILES = N // P
+
+GAMMA = (1.0 - math.exp(math.log(2.0**-5)), 1.0 - math.exp(math.log(2.0**-9)))
+
+FAR = PACK
+
+GROUP = 8
+AHEAD = 4
+
+FLOPS = 2 * 2 * D * PAIRS * CHUNK * CHUNK * (CHUNKS * (CHUNKS + 1) // 2)
+
+
+def tile_multiscaleretention_pb_t_kernel(tc, q_rot, k_scaled, v, out):
+    nc = tc.nc
+    flat_inputs = {
+        "k": k_scaled.flatten_outer_dims(),
+        "q": q_rot.flatten_outer_dims(),
+        "v": v.flatten_outer_dims(),
+    }
+    out_flat = out.flatten_outer_dims()
+
+    with ExitStack() as ctx:
+        ctx.enter_context(tc.manual_schedule())
+        consts = ctx.enter_context(tc.tile_pool(name="consts", bufs=1))
+        inputs = ctx.enter_context(tc.tile_pool(name="inputs", bufs=1))
+        turned_pool = ctx.enter_context(tc.tile_pool(name="turned", bufs=2))
+        values_pool = ctx.enter_context(tc.tile_pool(name="values", bufs=2))
+        work = ctx.enter_context(tc.tile_pool(name="work", bufs=2))
+        results = ctx.enter_context(tc.tile_pool(name="results", bufs=3))
+        psum_turn = ctx.enter_context(tc.psum_pool(name="psum_turn", bufs=1))
+        psum_sim = ctx.enter_context(tc.psum_pool(name="psum_sim", bufs=AHEAD + 1))
+        psum_acc = ctx.enter_context(tc.psum_pool(name="psum_acc", bufs=2))
+
+        rows = {}
+        for pair in range(PAIRS):
+            for chunk in range(CHUNKS):
+                first_row = pair * N + chunk * CHUNK
+                for which in ("k", "q", "v"):
+                    loaded = inputs.tile(
+                        [P, PACK, D], BF16, name="%s_rows_%d_%d" % (which, pair, chunk)
+                    )
+                    nc.sync.dma_start(
+                        out=loaded[:],
+                        in_=flat_inputs[which][first_row : first_row + CHUNK, :].rearrange(
+                            "(t p) d -> p t d" if which == "q" else "(p t) d -> p t d", p=P
+                        ),
+                    )
+                    rows[(which, pair, chunk)] = loaded
+
+        bank_pattern = [[1, P], [-1, PACK]]
+        distance_int = consts.tile([P, P, PACK], I32)
+        nc.gpsimd.iota(distance_int[:], pattern=bank_pattern, base=0, channel_multiplier=-PACK)
+        identity = consts.tile([P, P], BF16)
+        make_identity(nc, identity[:])
+        distance = consts.tile([P, P, PACK], F32)
+        nc.vector.tensor_copy(out=distance[:], in_=distance_int[:])
+        decay = []
+        for head in range(H):
+            near = consts.tile([P, P, PACK], F32, name="near_%d" % head)
+            nc.scalar.activation(
+                out=near[:],
+                in_=distance[:],
+                func=mybir.ActivationFunctionType.Exp,
+                scale=math.log(GAMMA[head]),
+            )
+            head_masks = consts.tile([P, FAR + 1, P, PACK], F32, name="masks_%d" % head)
+            for ahead in range(FAR + 1):
+                nc.vector.tensor_scalar_mul(
+                    out=head_masks[:, ahead, :, :],
+                    in0=near[:],
+                    scalar1=GAMMA[head] ** (P * ahead),
+                )
+            for ahead in range(FAR):
+                nc.gpsimd.affine_select(
+                    out=head_masks[:, ahead, :, :],
+                    in_=head_masks[:, ahead, :, :],
+                    pattern=bank_pattern,
+                    compare_op=mybir.AluOpType.is_ge,
+                    fill=0.0,
+                    base=P * ahead,
+                    channel_multiplier=-PACK,
+                )
+            decay.append(head_masks)
+
+        turned = {}
+        v_grouped = {}
+        v_quantised = {}
+
+        def turn(pair, chunk):
+            values = work.tile([P, D, PACK], BF16, align_bytes=64)
+            nc.scalar.copy(
+                out=values[:], in_=rows[("v", pair, chunk)][:].rearrange("p t d -> p d t")
+            )
+            v_grouped[(pair, chunk)] = values
+            turned_ps = psum_turn.tile([P, 2 * PACK, P], BF16)
+            for t in range(PACK):
+                nc.tensor.transpose(
+                    turned_ps[:, t, :], rows[("k", pair, chunk)][:, t, :], identity[:]
+                )
+            for t in range(PACK):
+                nc.tensor.transpose(
+                    turned_ps[:, PACK + t, :], rows[("q", pair, chunk)][:, t, :], identity[:]
+                )
+            kq = turned_pool.tile([P, 2 * PACK, P], BF16, name="turned_%d" % chunk)
+            nc.scalar.copy(out=kq[:], in_=turned_ps[:])
+            turned[(pair, chunk)] = kq
+
+        def quantise_values(pair, chunk):
+            v_codes = values_pool.tile([P, D], U32, name="v_codes_%d" % chunk, align_bytes=64)
+            v_scales = values_pool.tile([P, D], U8, name="v_scales_%d" % chunk, align_bytes=64)
+            nc.vector.quantize_mx(
+                out=v_codes[:].bitcast(FP8X4),
+                scales=v_scales[:],
+                in_=v_grouped[(pair, chunk)][:].rearrange("p d t -> p (d t)"),
+            )
+            v_quantised[(pair, chunk)] = (v_codes, v_scales)
+
+        def products(pair, chunk, slot, key_chunk):
+            sim_ps = psum_sim.tile([P, P, PACK], F32)
+            for t in range(PACK):
+                nc.tensor.matmul(
+                    out=sim_ps[:, :, t],
+                    lhsT=turned[(pair, key_chunk)][:, t, :],
+                    rhs=turned[(pair, chunk)][:, PACK + slot, :],
+                    start=True,
+                    stop=True,
+                )
+            return sim_ps
+
+        def mask(sim_ps, grouped_bank, pair, chunk, slot, key_chunk):
+            ahead = PACK * (chunk - key_chunk) + slot
+            nearest = min(ahead, FAR)
+            nc.vector.scalar_tensor_tensor(
+                out=grouped_bank,
+                in0=sim_ps[:],
+                scalar=GAMMA[pair % H] ** (P * (ahead - nearest)),
+                in1=decay[pair % H][:, nearest, :, :],
+                op0=mybir.AluOpType.mult,
+                op1=mybir.AluOpType.mult,
+            )
+
+        def store(acc, pair, chunk):
+            result = results.tile([P, PACK, D], F32)
+            nc.scalar.copy(out=result[:], in_=acc[:])
+            first_row = (pair // H) * N + chunk * CHUNK
+            first_column = (pair % H) * D
+            nc.scalar.dma_start(
+                out=out_flat[
+                    first_row : first_row + CHUNK, first_column : first_column + D
+                ].rearrange("(t p) d -> p t d", p=P),
+                in_=result[:],
+            )
+
+        accs = {}
+
+        def contract(grouped, members):
+            codes = work.tile([P, GROUP, P], U32, align_bytes=64)
+            scales = work.tile([P, GROUP, P], U8, align_bytes=64)
+            nc.vector.quantize_mx(
+                out=codes[:].rearrange("p b w -> p (b w)").bitcast(FP8X4),
+                scales=scales[:].rearrange("p b w -> p (b w)"),
+                in_=grouped[:].rearrange("p b w t -> p (b w t)"),
+            )
+            for place, (pair, chunk, slot, key_chunk) in enumerate(members):
+                if slot == 0 and key_chunk == 0:
+                    acc = psum_acc.tile([P, PACK, D], F32)
+                    accs[(pair, chunk)] = acc
+                v_codes, v_scales = v_quantised[(pair, key_chunk)]
+                nc.tensor.matmul_mx(
+                    out=accs[(pair, chunk)][:, slot, :],
+                    lhsT=codes[:, place, :].bitcast(FP8X4),
+                    lhsT_scale=scales[:, place, :],
+                    rhs=v_codes[:].bitcast(FP8X4),
+                    rhs_scale=v_scales[:],
+                    start=(key_chunk == 0),
+                    stop=(key_chunk == chunk),
+                )
+                if slot == PACK - 1 and key_chunk == chunk:
+                    store(accs[(pair, chunk)], pair, chunk)
+
+        banks = []
+        for pair in range(PAIRS):
+            for chunk in range(CHUNKS):
+                for slot in range(PACK):
+                    for key_chunk in range(chunk + 1):
+                        banks.append((pair, chunk, slot, key_chunk))
+
+        turn(0, 0)
+        quantise_values(0, 0)
+        sim_banks = {}
+        grouped = None
+        for tick in range(len(banks) + AHEAD):
+            if tick < len(banks):
+                sim_banks[tick] = products(*banks[tick])
+                pair, chunk, slot, key_chunk = banks[tick]
+                following = pair * CHUNKS + chunk + 1
+                if slot == 0 and key_chunk == 0 and following < PAIRS * CHUNKS:
+                    turn(following // CHUNKS, following % CHUNKS)
+            index = tick - AHEAD
+            if index < 0:
+                continue
+            pair, chunk, slot, key_chunk = banks[index]
+            full = grouped
+            if index % GROUP == 0:
+                grouped = work.tile([P, GROUP, P, PACK], BF16, align_bytes=64)
+            mask(sim_banks[index], grouped[:, index % GROUP, :, :], pair, chunk, slot, key_chunk)
+            following = pair * CHUNKS + chunk + 1
+            if slot == PACK - 1 and key_chunk == chunk and following < PAIRS * CHUNKS:
+                quantise_values(following // CHUNKS, following % CHUNKS)
+            if index % GROUP == 0 and index > 0:
+                contract(full, banks[index - GROUP : index])
+        contract(grouped, banks[len(banks) - GROUP :])

@@ -135,10 +135,10 @@ def tile_multiscaleretention_pb_t_kernel(tc, q_rot, k_scaled, v, out):
             v_quantised[(pair, chunk)] = (v_codes, v_scales)
 
         def products(pair, chunk, slot, key_chunk):
-            sim_ps = psum_sim.tile([P, P, PACK], F32)
+            sim_ps = psum_sim.tile([P, PACK, P], F32)
             for t in range(PACK):
                 nc.tensor.matmul(
-                    out=sim_ps[:, :, t],
+                    out=sim_ps[:, t, :],
                     lhsT=turned[(pair, key_chunk)][:, t, :],
                     rhs=turned[(pair, chunk)][:, PACK + slot, :],
                     start=True,
@@ -151,7 +151,7 @@ def tile_multiscaleretention_pb_t_kernel(tc, q_rot, k_scaled, v, out):
             nearest = min(ahead, FAR)
             nc.vector.scalar_tensor_tensor(
                 out=grouped_bank,
-                in0=sim_ps[:],
+                in0=sim_ps[:].rearrange("p t w -> p w t"),
                 scalar=GAMMA[pair % H] ** (P * (ahead - nearest)),
                 in1=decay[pair % H][:, nearest, :, :],
                 op0=mybir.AluOpType.mult,

@@ -6,7 +6,6 @@ from concourse.masks import make_identity
 
 BF16 = mybir.dt.bfloat16
 F32 = mybir.dt.float32
-I32 = mybir.dt.int32
 U32 = mybir.dt.uint32
 U8 = mybir.dt.uint8
 FP8X4 = mybir.dt.float8_e4m3fn_x4
@@ -24,7 +23,11 @@ GAMMA = (1.0 - math.exp(math.log(2.0**-5)), 1.0 - math.exp(math.log(2.0**-9)))
 FAR = PACK
 
 GROUP = 8
-AHEAD = 4
+AHEAD = 3
+TURN_LEAD = 6
+PASSES_PER_TICK = 2
+HEAD_1_TICK = 12
+SCALAR_PLACES = (2, 5)
 
 FLOPS = 2 * 2 * D * PAIRS * CHUNK * CHUNK * (CHUNKS * (CHUNKS + 1) // 2)
 
@@ -44,9 +47,12 @@ def tile_multiscaleretention_pb_t_kernel(tc, q_rot, k_scaled, v, out):
         inputs = ctx.enter_context(tc.tile_pool(name="inputs", bufs=1))
         turned_pool = ctx.enter_context(tc.tile_pool(name="turned", bufs=2))
         values_pool = ctx.enter_context(tc.tile_pool(name="values", bufs=2))
+        interleaved = ctx.enter_context(tc.tile_pool(name="interleaved", bufs=4))
         work = ctx.enter_context(tc.tile_pool(name="work", bufs=2))
+        grouped_pool = ctx.enter_context(tc.tile_pool(name="grouped", bufs=3))
+        moved_pool = ctx.enter_context(tc.tile_pool(name="moved", bufs=3))
         results = ctx.enter_context(tc.tile_pool(name="results", bufs=3))
-        psum_turn = ctx.enter_context(tc.psum_pool(name="psum_turn", bufs=1))
+        psum_scalar = ctx.enter_context(tc.psum_pool(name="psum_scalar", bufs=2))
         psum_sim = ctx.enter_context(tc.psum_pool(name="psum_sim", bufs=AHEAD + 1))
         psum_acc = ctx.enter_context(tc.psum_pool(name="psum_acc", bufs=2))
 
@@ -66,15 +72,19 @@ def tile_multiscaleretention_pb_t_kernel(tc, q_rot, k_scaled, v, out):
                     )
                     rows[(which, pair, chunk)] = loaded
 
-        bank_pattern = [[1, P], [-1, PACK]]
-        distance_int = consts.tile([P, P, PACK], I32)
-        nc.gpsimd.iota(distance_int[:], pattern=bank_pattern, base=0, channel_multiplier=-PACK)
+        distance = consts.tile([P, P, PACK], F32)
+        nc.gpsimd.iota(
+            distance[:],
+            pattern=[[1, P], [-1, PACK]],
+            base=0,
+            channel_multiplier=-PACK,
+            allow_small_or_imprecise_dtypes=True,
+        )
         identity = consts.tile([P, P], BF16)
         make_identity(nc, identity[:])
-        distance = consts.tile([P, P, PACK], F32)
-        nc.vector.tensor_copy(out=distance[:], in_=distance_int[:])
-        decay = []
-        for head in range(H):
+        decay = {}
+
+        def build_masks(head):
             near = consts.tile([P, P, PACK], F32, name="near_%d" % head)
             nc.scalar.activation(
                 out=near[:],
@@ -82,36 +92,29 @@ def tile_multiscaleretention_pb_t_kernel(tc, q_rot, k_scaled, v, out):
                 func=mybir.ActivationFunctionType.Exp,
                 scale=math.log(GAMMA[head]),
             )
-            head_masks = consts.tile([P, FAR + 1, P, PACK], F32, name="masks_%d" % head)
-            for ahead in range(FAR + 1):
-                nc.vector.tensor_scalar_mul(
-                    out=head_masks[:, ahead, :, :],
-                    in0=near[:],
-                    scalar1=GAMMA[head] ** (P * ahead),
-                )
+            head_masks = []
             for ahead in range(FAR):
-                nc.gpsimd.affine_select(
-                    out=head_masks[:, ahead, :, :],
-                    in_=head_masks[:, ahead, :, :],
-                    pattern=bank_pattern,
-                    compare_op=mybir.AluOpType.is_ge,
-                    fill=0.0,
-                    base=P * ahead,
-                    channel_multiplier=-PACK,
+                selected = consts.tile([P, P, PACK], F32, name="mask_%d_%d" % (head, ahead))
+                nc.vector.scalar_tensor_tensor(
+                    out=selected[:],
+                    in0=distance[:],
+                    scalar=float(-P * ahead),
+                    in1=near[:],
+                    op0=mybir.AluOpType.is_ge,
+                    op1=mybir.AluOpType.mult,
                 )
-            decay.append(head_masks)
+                head_masks.append(selected)
+            head_masks.append(near)
+            decay[head] = head_masks
+
+        build_masks(0)
 
         turned = {}
         v_grouped = {}
         v_quantised = {}
 
         def turn(pair, chunk):
-            values = work.tile([P, D, PACK], BF16, align_bytes=64)
-            nc.scalar.copy(
-                out=values[:], in_=rows[("v", pair, chunk)][:].rearrange("p t d -> p d t")
-            )
-            v_grouped[(pair, chunk)] = values
-            turned_ps = psum_turn.tile([P, 2 * PACK, P], BF16)
+            turned_ps = psum_scalar.tile([P, 2 * PACK, P], BF16, name="scalar_bank")
             for t in range(PACK):
                 nc.tensor.transpose(
                     turned_ps[:, t, :], rows[("k", pair, chunk)][:, t, :], identity[:]
@@ -123,6 +126,11 @@ def tile_multiscaleretention_pb_t_kernel(tc, q_rot, k_scaled, v, out):
             kq = turned_pool.tile([P, 2 * PACK, P], BF16, name="turned_%d" % chunk)
             nc.scalar.copy(out=kq[:], in_=turned_ps[:])
             turned[(pair, chunk)] = kq
+            values = interleaved.tile([P, D, PACK], BF16, align_bytes=64)
+            nc.scalar.copy(
+                out=values[:], in_=rows[("v", pair, chunk)][:].rearrange("p t d -> p d t")
+            )
+            v_grouped[(pair, chunk)] = values
 
         def quantise_values(pair, chunk):
             v_codes = values_pool.tile([P, D], U32, name="v_codes_%d" % chunk, align_bytes=64)
@@ -134,36 +142,26 @@ def tile_multiscaleretention_pb_t_kernel(tc, q_rot, k_scaled, v, out):
             )
             v_quantised[(pair, chunk)] = (v_codes, v_scales)
 
-        def products(pair, chunk, slot, key_chunk):
-            sim_ps = psum_sim.tile([P, PACK, P], F32)
+        def products(bank_ps, pair, chunk, slot, key_chunk):
             for t in range(PACK):
                 nc.tensor.matmul(
-                    out=sim_ps[:, t, :],
+                    out=bank_ps[:, t, :],
                     lhsT=turned[(pair, key_chunk)][:, t, :],
                     rhs=turned[(pair, chunk)][:, PACK + slot, :],
                     start=True,
                     stop=True,
                 )
-            return sim_ps
 
-        def mask(sim_ps, grouped_bank, pair, chunk, slot, key_chunk):
+        def mask_of(pair, chunk, slot, key_chunk):
             ahead = PACK * (chunk - key_chunk) + slot
-            nearest = min(ahead, FAR)
-            nc.vector.scalar_tensor_tensor(
-                out=grouped_bank,
-                in0=sim_ps[:].rearrange("p t w -> p w t"),
-                scalar=GAMMA[pair % H] ** (P * (ahead - nearest)),
-                in1=decay[pair % H][:, nearest, :, :],
-                op0=mybir.AluOpType.mult,
-                op1=mybir.AluOpType.mult,
-            )
+            return decay[pair % H][min(ahead, FAR)], GAMMA[pair % H] ** (P * ahead)
 
         def store(acc, pair, chunk):
             result = results.tile([P, PACK, D], F32)
             nc.scalar.copy(out=result[:], in_=acc[:])
             first_row = (pair // H) * N + chunk * CHUNK
             first_column = (pair % H) * D
-            nc.scalar.dma_start(
+            nc.sync.dma_start(
                 out=out_flat[
                     first_row : first_row + CHUNK, first_column : first_column + D
                 ].rearrange("(t p) d -> p t d", p=P),
@@ -172,7 +170,9 @@ def tile_multiscaleretention_pb_t_kernel(tc, q_rot, k_scaled, v, out):
 
         accs = {}
 
-        def contract(grouped, members):
+        pending = []
+
+        def quantise(grouped, members):
             codes = work.tile([P, GROUP, P], U32, align_bytes=64)
             scales = work.tile([P, GROUP, P], U8, align_bytes=64)
             nc.vector.quantize_mx(
@@ -180,7 +180,11 @@ def tile_multiscaleretention_pb_t_kernel(tc, q_rot, k_scaled, v, out):
                 scales=scales[:].rearrange("p b w -> p (b w)"),
                 in_=grouped[:].rearrange("p b w t -> p (b w t)"),
             )
-            for place, (pair, chunk, slot, key_chunk) in enumerate(members):
+            for place, member in enumerate(members):
+                pending.append((codes, scales, place, member))
+
+        def contract(count):
+            for codes, scales, place, (pair, chunk, slot, key_chunk) in pending[:count]:
                 if slot == 0 and key_chunk == 0:
                     acc = psum_acc.tile([P, PACK, D], F32)
                     accs[(pair, chunk)] = acc
@@ -196,6 +200,7 @@ def tile_multiscaleretention_pb_t_kernel(tc, q_rot, k_scaled, v, out):
                 )
                 if slot == PACK - 1 and key_chunk == chunk:
                     store(accs[(pair, chunk)], pair, chunk)
+            pending[:] = pending[count:]
 
         banks = []
         for pair in range(PAIRS):
@@ -203,29 +208,86 @@ def tile_multiscaleretention_pb_t_kernel(tc, q_rot, k_scaled, v, out):
                 for slot in range(PACK):
                     for key_chunk in range(chunk + 1):
                         banks.append((pair, chunk, slot, key_chunk))
+        groups = len(banks) // GROUP
 
-        turn(0, 0)
-        quantise_values(0, 0)
-        sim_banks = {}
-        grouped = None
-        for tick in range(len(banks) + AHEAD):
-            if tick < len(banks):
-                sim_banks[tick] = products(*banks[tick])
-                pair, chunk, slot, key_chunk = banks[tick]
-                following = pair * CHUNKS + chunk + 1
-                if slot == 0 and key_chunk == 0 and following < PAIRS * CHUNKS:
-                    turn(following // CHUNKS, following % CHUNKS)
-            index = tick - AHEAD
-            if index < 0:
+        def by_scalar(index):
+            return index >= GROUP and index % GROUP in SCALAR_PLACES
+
+        order = []
+        for group in range(groups):
+            for place in range(GROUP):
+                index = group * GROUP + place
+                if not by_scalar(index):
+                    order.append(index)
+                if index + GROUP < len(banks) and by_scalar(index + GROUP):
+                    order.append(index + GROUP)
+
+        group_tiles = {}
+
+        def place_of(index):
+            group = index // GROUP
+            if group not in group_tiles:
+                grouped = grouped_pool.tile([P, GROUP, P, PACK], BF16, align_bytes=64)
+                group_tiles[group] = grouped
+            return group_tiles[group][:, index % GROUP, :, :]
+
+        turned_steps = 0
+        quantised_steps = 0
+        vector_banks = {}
+        contracted = 0
+        for tick in range(len(order) + AHEAD):
+            last_needed = order[min(tick + TURN_LEAD, len(order) - 1)]
+            while turned_steps <= banks[last_needed][0] * CHUNKS + banks[last_needed][1]:
+                turn(turned_steps // CHUNKS, turned_steps % CHUNKS)
+                turned_steps += 1
+            if tick == HEAD_1_TICK:
+                build_masks(1)
+            if tick < len(order):
+                index = order[tick]
+                matrix, factor = mask_of(*banks[index])
+                if by_scalar(index):
+                    scalar_bank = psum_scalar.tile([P, PACK, P], F32, name="scalar_bank")
+                    products(scalar_bank, *banks[index])
+                    moved = moved_pool.tile([P, P, PACK], F32)
+                    nc.scalar.activation(
+                        out=moved[:],
+                        in_=scalar_bank[:].rearrange("p t w -> p w t"),
+                        func=mybir.ActivationFunctionType.Copy,
+                        scale=factor,
+                    )
+                    nc.gpsimd.tensor_tensor(
+                        out=place_of(index),
+                        in0=moved[:],
+                        in1=matrix[:],
+                        op=mybir.AluOpType.mult,
+                    )
+                else:
+                    sim_ps = psum_sim.tile([P, PACK, P], F32)
+                    products(sim_ps, *banks[index])
+                    vector_banks[index] = sim_ps
+            if tick < AHEAD:
                 continue
-            pair, chunk, slot, key_chunk = banks[index]
-            full = grouped
-            if index % GROUP == 0:
-                grouped = work.tile([P, GROUP, P, PACK], BF16, align_bytes=64)
-            mask(sim_banks[index], grouped[:, index % GROUP, :, :], pair, chunk, slot, key_chunk)
-            following = pair * CHUNKS + chunk + 1
-            if slot == PACK - 1 and key_chunk == chunk and following < PAIRS * CHUNKS:
-                quantise_values(following // CHUNKS, following % CHUNKS)
-            if index % GROUP == 0 and index > 0:
-                contract(full, banks[index - GROUP : index])
-        contract(grouped, banks[len(banks) - GROUP :])
+            index = order[tick - AHEAD]
+            if by_scalar(index):
+                continue
+            matrix, factor = mask_of(*banks[index])
+            nc.vector.scalar_tensor_tensor(
+                out=place_of(index),
+                in0=vector_banks[index][:].rearrange("p t w -> p w t"),
+                scalar=factor,
+                in1=matrix[:],
+                op0=mybir.AluOpType.mult,
+                op1=mybir.AluOpType.mult,
+            )
+            group = index // GROUP
+            if index % GROUP == 0 and group > 0:
+                quantise(group_tiles[group - 1], banks[index - GROUP : index])
+            else:
+                contract(PASSES_PER_TICK)
+            if index % GROUP == 1:
+                pair, chunk, slot, key_chunk = banks[group * GROUP + GROUP - 1]
+                while quantised_steps <= pair * CHUNKS + chunk:
+                    quantise_values(quantised_steps // CHUNKS, quantised_steps % CHUNKS)
+                    quantised_steps += 1
+        quantise(group_tiles[groups - 1], banks[len(banks) - GROUP :])
+        contract(len(pending))

@@ -6,30 +6,46 @@ from concourse.masks import make_identity
 
 BF16 = mybir.dt.bfloat16
 F32 = mybir.dt.float32
+I32 = mybir.dt.int32
 U32 = mybir.dt.uint32
 U8 = mybir.dt.uint8
 FP8X4 = mybir.dt.float8_e4m3fn_x4
 
 P = 128
 PACK = 4
+QUADS = 4
+QUAD = P // QUADS
 CHUNK = P * PACK
 B, H, N, D = 2, 2, 2048, 128
-PAIRS = B * H
 CHUNKS = N // CHUNK
-TILES = N // P
+STEPS = H * CHUNKS
+LAST = QUADS - 1
 
 GAMMA = (1.0 - math.exp(math.log(2.0**-5)), 1.0 - math.exp(math.log(2.0**-9)))
 
-FAR = PACK
-
 GROUP = 8
 AHEAD = 3
-TURN_LEAD = 6
-PASSES_PER_TICK = 2
-HEAD_1_TICK = 12
+FIRST_VALUES = 3
+EMPTYING = 3
+CHORE_LEAD = 16
+SETS = 3
+LOAD_LEAD = 2
+PASSES_PER_TICK = 3
+POWERS_TICK, MASKS_TICK = 24, 30
 SCALAR_PLACES = (2, 5)
 
-FLOPS = 2 * 2 * D * PAIRS * CHUNK * CHUNK * (CHUNKS * (CHUNKS + 1) // 2)
+PAD = P - QUAD
+WORDS = D + D // 4
+
+FLOPS = 2 * 2 * D * B * H * CHUNK * CHUNK * (CHUNKS * (CHUNKS + 1) // 2)
+
+SHARED_TILES = (2, 0, 1)
+
+SHARED_RUNS = {
+    0: (slice(0, 1), slice(1, 2), slice(2, 4)),
+    1: (slice(0, 2), slice(2, 4)),
+    2: (slice(0, 3), slice(3, 4)),
+}
 
 
 def tile_multiscaleretention_pb_t_kernel(tc, q_rot, k_scaled, v, out):
@@ -45,32 +61,55 @@ def tile_multiscaleretention_pb_t_kernel(tc, q_rot, k_scaled, v, out):
         ctx.enter_context(tc.manual_schedule())
         consts = ctx.enter_context(tc.tile_pool(name="consts", bufs=1))
         inputs = ctx.enter_context(tc.tile_pool(name="inputs", bufs=1))
-        turned_pool = ctx.enter_context(tc.tile_pool(name="turned", bufs=2))
         values_pool = ctx.enter_context(tc.tile_pool(name="values", bufs=2))
-        interleaved = ctx.enter_context(tc.tile_pool(name="interleaved", bufs=4))
-        work = ctx.enter_context(tc.tile_pool(name="work", bufs=2))
+        interleaved = ctx.enter_context(tc.tile_pool(name="interleaved", bufs=6))
+        work = ctx.enter_context(tc.tile_pool(name="work", bufs=3))
         grouped_pool = ctx.enter_context(tc.tile_pool(name="grouped", bufs=3))
         moved_pool = ctx.enter_context(tc.tile_pool(name="moved", bufs=3))
         results = ctx.enter_context(tc.tile_pool(name="results", bufs=3))
         psum_scalar = ctx.enter_context(tc.psum_pool(name="psum_scalar", bufs=2))
         psum_sim = ctx.enter_context(tc.psum_pool(name="psum_sim", bufs=AHEAD + 1))
-        psum_acc = ctx.enter_context(tc.psum_pool(name="psum_acc", bufs=2))
+        psum_acc = ctx.enter_context(tc.psum_pool(name="psum_acc", bufs=1))
 
         rows = {}
-        for pair in range(PAIRS):
-            for chunk in range(CHUNKS):
-                first_row = pair * N + chunk * CHUNK
-                for which in ("k", "q", "v"):
+
+        def load(step):
+            head, chunk = divmod(step, CHUNKS)
+            for which in ("k", "q", "v"):
+                for batch in range(B):
+                    first_row = (batch * H + head) * N + chunk * CHUNK
                     loaded = inputs.tile(
-                        [P, PACK, D], BF16, name="%s_rows_%d_%d" % (which, pair, chunk)
+                        [P, PACK, D], BF16, name="%s_rows_%d_%d" % (which, batch, step)
                     )
-                    nc.sync.dma_start(
-                        out=loaded[:],
-                        in_=flat_inputs[which][first_row : first_row + CHUNK, :].rearrange(
-                            "(t p) d -> p t d" if which == "q" else "(p t) d -> p t d", p=P
-                        ),
-                    )
-                    rows[(which, pair, chunk)] = loaded
+                    whole = flat_inputs[which][first_row : first_row + CHUNK, :]
+                    if which == "q":
+                        nc.sync.dma_start(
+                            out=loaded[:], in_=whole.rearrange("(t p) d -> p t d", p=P)
+                        )
+                    elif batch == 1:
+                        nc.sync.dma_start(
+                            out=loaded[:], in_=whole.rearrange("(p t) d -> p t d", p=P)
+                        )
+                    else:
+                        for quadrant in range(QUADS):
+                            first_key = P * (LAST - quadrant)
+                            nc.sync.dma_start(
+                                out=loaded[QUAD * quadrant : QUAD * (quadrant + 1), :, :],
+                                in_=whole[first_key : first_key + P, :].rearrange(
+                                    "(p t) d -> p t d", p=QUAD
+                                ),
+                            )
+                    rows[(which, batch, step)] = loaded
+
+        for step in range(LOAD_LEAD):
+            load(step)
+
+        warm = consts.tile([P, 1], F32)
+        nc.vector.memset(warm[:], 0.0)
+        warmed = consts.tile([P, 1], F32)
+        nc.scalar.activation(
+            out=warmed[:], in_=warm[:], func=mybir.ActivationFunctionType.Exp
+        )
 
         distance = consts.tile([P, P, PACK], F32)
         nc.gpsimd.iota(
@@ -82,94 +121,164 @@ def tile_multiscaleretention_pb_t_kernel(tc, q_rot, k_scaled, v, out):
         )
         identity = consts.tile([P, P], BF16)
         make_identity(nc, identity[:])
-        decay = {}
+
+        turned_back = consts.tile([P, 1], F32)
+        for quadrant in range(QUADS):
+            nc.vector.memset(
+                turned_back[QUAD * quadrant : QUAD * (quadrant + 1), :],
+                float(2 * P * quadrant),
+            )
+        first_causal = consts.tile([P, 1], F32)
+        nc.vector.tensor_scalar_mul(out=first_causal[:], in0=turned_back[:], scalar1=-1.0)
+        exponents = []
+        for head in range(H):
+            head_exponents = consts.tile([P, 1], F32, name="exponents_%d" % head)
+            nc.vector.tensor_scalar(
+                out=head_exponents[:],
+                in0=turned_back[:],
+                scalar1=float(-P * LAST),
+                scalar2=math.log(GAMMA[head]),
+                op0=mybir.AluOpType.add,
+                op1=mybir.AluOpType.mult,
+            )
+            exponents.append(head_exponents)
+
+        earlier_masks = {}
+        last_masks = {}
+        shared_masks = {}
+
+        def build_powers(head):
+            for batch in range(B):
+                powers = consts.tile([P, P, PACK], F32, name="powers_%d_%d" % (head, batch))
+                nc.scalar.activation(
+                    out=powers[:],
+                    in_=distance[:],
+                    func=mybir.ActivationFunctionType.Exp,
+                    bias=exponents[head][:] if batch == 0 else 0.0,
+                    scale=math.log(GAMMA[head]),
+                )
+                earlier_masks[(head, batch)] = powers
 
         def build_masks(head):
-            near = consts.tile([P, P, PACK], F32, name="near_%d" % head)
-            nc.scalar.activation(
-                out=near[:],
-                in_=distance[:],
-                func=mybir.ActivationFunctionType.Exp,
-                scale=math.log(GAMMA[head]),
-            )
-            head_masks = []
-            for ahead in range(FAR):
-                selected = consts.tile([P, P, PACK], F32, name="mask_%d_%d" % (head, ahead))
+            for batch in range(B):
+                last_mask = consts.tile([P, P, PACK], F32, name="last_%d_%d" % (head, batch))
                 nc.vector.scalar_tensor_tensor(
-                    out=selected[:],
+                    out=last_mask[:],
                     in0=distance[:],
-                    scalar=float(-P * ahead),
-                    in1=near[:],
+                    scalar=first_causal[:] if batch == 0 else float(-P * LAST),
+                    in1=earlier_masks[(head, batch)][:],
                     op0=mybir.AluOpType.is_ge,
                     op1=mybir.AluOpType.mult,
                 )
-                head_masks.append(selected)
-            head_masks.append(near)
-            decay[head] = head_masks
+                last_masks[(head, batch)] = last_mask
+            for tile_0 in SHARED_TILES:
+                shared_mask = consts.tile(
+                    [P, P, PACK], F32, name="shared_%d_%d" % (head, tile_0)
+                )
+                for quadrants in SHARED_RUNS[tile_0]:
+                    batch = 0 if quadrants.start <= tile_0 else 1
+                    partitions = slice(QUAD * quadrants.start, QUAD * quadrants.stop)
+                    nc.vector.tensor_copy(
+                        out=shared_mask[partitions, :, :],
+                        in_=last_masks[(head, batch)][partitions, :, :],
+                    )
+                shared_masks[(head, tile_0)] = shared_mask
 
+        build_powers(0)
         build_masks(0)
 
         turned = {}
+
+        def border(step):
+            for batch in range(B):
+                kq = consts.tile([P, 2 * PACK, PAD + P], BF16, name="turned_%d_%d" % (batch, step))
+                zeros = slice(P, PAD + P) if batch == 0 else slice(0, PAD)
+                nc.gpsimd.memset(kq[:, 0:PACK, zeros], 0.0)
+                turned[(batch, step)] = kq
+
+        for step in range(LOAD_LEAD):
+            border(step)
+
+        moved_values = []
+        for number in range(SETS):
+            value_set = consts.tile(
+                [P, B, LAST, WORDS], U32, name="moved_values_%d" % number, align_bytes=64
+            )
+            nc.gpsimd.memset(value_set[:], 0)
+            moved_values.append(value_set)
+        for step in range(LOAD_LEAD, STEPS):
+            border(step)
+
         v_grouped = {}
         v_quantised = {}
 
-        def turn(pair, chunk):
+        def turn(batch, step):
             turned_ps = psum_scalar.tile([P, 2 * PACK, P], BF16, name="scalar_bank")
             for t in range(PACK):
                 nc.tensor.transpose(
-                    turned_ps[:, t, :], rows[("k", pair, chunk)][:, t, :], identity[:]
+                    turned_ps[:, t, :], rows[("k", batch, step)][:, t, :], identity[:]
                 )
             for t in range(PACK):
                 nc.tensor.transpose(
-                    turned_ps[:, PACK + t, :], rows[("q", pair, chunk)][:, t, :], identity[:]
+                    turned_ps[:, PACK + t, :], rows[("q", batch, step)][:, t, :], identity[:]
                 )
-            kq = turned_pool.tile([P, 2 * PACK, P], BF16, name="turned_%d" % chunk)
-            nc.scalar.copy(out=kq[:], in_=turned_ps[:])
-            turned[(pair, chunk)] = kq
+            kq = turned[(batch, step)]
+            data = slice(0, P) if batch == 0 else slice(PAD, PAD + P)
+            nc.scalar.copy(out=kq[:, :, data], in_=turned_ps[:])
+
+        def interleave(batch, step):
             values = interleaved.tile([P, D, PACK], BF16, align_bytes=64)
             nc.scalar.copy(
-                out=values[:], in_=rows[("v", pair, chunk)][:].rearrange("p t d -> p d t")
+                out=values[:], in_=rows[("v", batch, step)][:].rearrange("p t d -> p d t")
             )
-            v_grouped[(pair, chunk)] = values
+            v_grouped[(batch, step)] = values
 
-        def quantise_values(pair, chunk):
-            v_codes = values_pool.tile([P, D], U32, name="v_codes_%d" % chunk, align_bytes=64)
-            v_scales = values_pool.tile([P, D], U8, name="v_scales_%d" % chunk, align_bytes=64)
+        def quantise_values(batch, step):
+            words = values_pool.tile(
+                [P, WORDS], U32, name="values_%d_%d" % (batch, step % CHUNKS), align_bytes=64
+            )
             nc.vector.quantize_mx(
-                out=v_codes[:].bitcast(FP8X4),
-                scales=v_scales[:],
-                in_=v_grouped[(pair, chunk)][:].rearrange("p d t -> p (d t)"),
+                out=words[:, 0:D].bitcast(FP8X4),
+                scales=words[:, D:WORDS].bitcast(U8),
+                in_=v_grouped[(batch, step)][:].rearrange("p d t -> p (d t)"),
             )
-            v_quantised[(pair, chunk)] = (v_codes, v_scales)
-
-        def products(bank_ps, pair, chunk, slot, key_chunk):
-            for t in range(PACK):
-                nc.tensor.matmul(
-                    out=bank_ps[:, t, :],
-                    lhsT=turned[(pair, key_chunk)][:, t, :],
-                    rhs=turned[(pair, chunk)][:, PACK + slot, :],
-                    start=True,
-                    stop=True,
+            v_quantised[(batch, step)] = words
+            for tiles in range(1, QUADS):
+                far_end = slice(P - QUAD * tiles, P)
+                near_end = slice(0, QUAD * tiles)
+                source, target = (far_end, near_end) if batch == 0 else (near_end, far_end)
+                nc.sync.dma_start(
+                    out=moved_values[step % SETS][target, batch, tiles - 1, :].bitcast(I32),
+                    in_=words[source, :].bitcast(I32),
                 )
 
-        def mask_of(pair, chunk, slot, key_chunk):
-            ahead = PACK * (chunk - key_chunk) + slot
-            return decay[pair % H][min(ahead, FAR)], GAMMA[pair % H] ** (P * ahead)
+        def products(bank_ps, bank):
+            for t in range(PACK):
+                for number, (batch, step, slot, key_step) in enumerate(bank["parts"]):
+                    tiles = QUADS if key_step < step else slot + 1
+                    start = P - QUAD * tiles if batch == 0 else QUAD * tiles - (P - PAD)
+                    first = 0 if batch == 0 else PAD
+                    nc.tensor.matmul(
+                        out=bank_ps[:, t, :],
+                        lhsT=turned[(batch, key_step)][:, t, start : start + P],
+                        rhs=turned[(batch, step)][:, PACK + slot, first : first + P],
+                        start=(number == 0),
+                        stop=(number == len(bank["parts"]) - 1),
+                    )
 
-        def store(acc, pair, chunk):
-            result = results.tile([P, PACK, D], F32)
+        def store(acc, batch, step):
+            head, chunk = divmod(step, CHUNKS)
+            result = results.tile([P, QUADS, D], F32)
             nc.scalar.copy(out=result[:], in_=acc[:])
-            first_row = (pair // H) * N + chunk * CHUNK
-            first_column = (pair % H) * D
-            nc.sync.dma_start(
+            first_row = batch * N + chunk * CHUNK
+            nc.scalar.dma_start(
                 out=out_flat[
-                    first_row : first_row + CHUNK, first_column : first_column + D
+                    first_row : first_row + CHUNK, head * D : (head + 1) * D
                 ].rearrange("(t p) d -> p t d", p=P),
                 in_=result[:],
             )
 
         accs = {}
-
         pending = []
 
         def quantise(grouped, members):
@@ -180,34 +289,72 @@ def tile_multiscaleretention_pb_t_kernel(tc, q_rot, k_scaled, v, out):
                 scales=scales[:].rearrange("p b w -> p (b w)"),
                 in_=grouped[:].rearrange("p b w t -> p (b w t)"),
             )
-            for place, member in enumerate(members):
-                pending.append((codes, scales, place, member))
+            for place, bank in enumerate(members):
+                for part in bank["parts"]:
+                    pending.append((codes[:, place, :], scales[:, place, :], part))
 
-        def contract(count):
-            for codes, scales, place, (pair, chunk, slot, key_chunk) in pending[:count]:
-                if slot == 0 and key_chunk == 0:
-                    acc = psum_acc.tile([P, PACK, D], F32)
-                    accs[(pair, chunk)] = acc
-                v_codes, v_scales = v_quantised[(pair, key_chunk)]
+        passes_left = {}
+
+        stored_at = {0: -EMPTYING, 1: -EMPTYING}
+
+        def contract(count, tick):
+            issued = 0
+            for codes, scales, (batch, step, slot, key_step) in pending[:count]:
+                if (batch, step) not in accs:
+                    if tick < stored_at[batch] + EMPTYING:
+                        break
+                    acc = psum_acc.tile([P, QUADS, D], F32, name="acc_%d" % batch)
+                    accs[(batch, step)] = acc
+                    passes_left[(batch, step)] = QUADS
+                if key_step < step or slot == LAST:
+                    words = v_quantised[(batch, key_step)][:]
+                else:
+                    words = moved_values[step % SETS][:, batch, slot, :]
                 nc.tensor.matmul_mx(
-                    out=accs[(pair, chunk)][:, slot, :],
-                    lhsT=codes[:, place, :].bitcast(FP8X4),
-                    lhsT_scale=scales[:, place, :],
-                    rhs=v_codes[:].bitcast(FP8X4),
-                    rhs_scale=v_scales[:],
-                    start=(key_chunk == 0),
-                    stop=(key_chunk == chunk),
+                    out=accs[(batch, step)][:, slot, :],
+                    lhsT=codes.bitcast(FP8X4),
+                    lhsT_scale=scales,
+                    rhs=words[:, 0:D].bitcast(FP8X4),
+                    rhs_scale=words[:, D:WORDS].bitcast(U8),
+                    start=(key_step % CHUNKS == 0),
+                    stop=(key_step == step),
                 )
-                if slot == PACK - 1 and key_chunk == chunk:
-                    store(accs[(pair, chunk)], pair, chunk)
-            pending[:] = pending[count:]
+                if key_step == step:
+                    passes_left[(batch, step)] -= 1
+                    if passes_left[(batch, step)] == 0:
+                        store(accs[(batch, step)], batch, step)
+                        stored_at[batch] = tick
+                issued += 1
+            pending[:] = pending[issued:]
 
         banks = []
-        for pair in range(PAIRS):
-            for chunk in range(CHUNKS):
-                for slot in range(PACK):
-                    for key_chunk in range(chunk + 1):
-                        banks.append((pair, chunk, slot, key_chunk))
+
+        def add(step, masks, key, power, parts):
+            banks.append(
+                {
+                    "step": step,
+                    "masks": masks,
+                    "key": key,
+                    "power": power,
+                    "parts": parts,
+                }
+            )
+
+        def add_earlier(batch, step, slot):
+            for key_step in range(step - step % CHUNKS, step):
+                power = CHUNK * (step - key_step) + P * slot
+                add(step, earlier_masks, batch, power, [(batch, step, slot, key_step)])
+
+        for step in range(STEPS):
+            for tile_0 in SHARED_TILES:
+                tile_1 = LAST - 1 - tile_0
+                add_earlier(0, step, tile_0)
+                add_earlier(1, step, tile_1)
+                parts = [(0, step, tile_0, step), (1, step, tile_1, step)]
+                add(step, shared_masks, tile_0, P * LAST, parts)
+            for batch in range(B):
+                add_earlier(batch, step, LAST)
+                add(step, last_masks, batch, P * LAST, [(batch, step, LAST, step)])
         groups = len(banks) // GROUP
 
         def by_scalar(index):
@@ -215,12 +362,15 @@ def tile_multiscaleretention_pb_t_kernel(tc, q_rot, k_scaled, v, out):
 
         order = []
         for group in range(groups):
-            for place in range(GROUP):
-                index = group * GROUP + place
-                if not by_scalar(index):
-                    order.append(index)
-                if index + GROUP < len(banks) and by_scalar(index + GROUP):
-                    order.append(index + GROUP)
+            own = [i for i in range(group * GROUP, (group + 1) * GROUP) if not by_scalar(i)]
+            early = range((group + 1) * GROUP, min((group + 2) * GROUP, len(banks)))
+            early = [i for i in early if by_scalar(i)]
+            split = len(own) - len(early) + 1
+            order.extend(own[:split])
+            for index, follower in zip(early, own[split:] + [None]):
+                order.append(index)
+                if follower is not None:
+                    order.append(follower)
 
         group_tiles = {}
 
@@ -231,51 +381,72 @@ def tile_multiscaleretention_pb_t_kernel(tc, q_rot, k_scaled, v, out):
                 group_tiles[group] = grouped
             return group_tiles[group][:, index % GROUP, :, :]
 
-        turned_steps = 0
-        quantised_steps = 0
+        loaded_steps = LOAD_LEAD
+        chores = []
+        for step in range(STEPS):
+            chores.extend((step, turn, batch) for batch in range(B))
+            chores.extend((step, interleave, batch) for batch in range(B))
+        chores_done = 0
+
+        def do_chores(due):
+            done = max(due, 0)
+            for step, chore, batch in chores[:done]:
+                chore(batch, step)
+            chores[:done] = []
+            return done
+
+        quantised_halves = 0
         vector_banks = {}
-        contracted = 0
         for tick in range(len(order) + AHEAD):
-            last_needed = order[min(tick + TURN_LEAD, len(order) - 1)]
-            while turned_steps <= banks[last_needed][0] * CHUNKS + banks[last_needed][1]:
-                turn(turned_steps // CHUNKS, turned_steps % CHUNKS)
-                turned_steps += 1
-            if tick == HEAD_1_TICK:
+            now = banks[order[min(tick, len(order) - 1)]]["step"]
+            coming = banks[order[min(tick + CHORE_LEAD, len(order) - 1)]]["step"]
+            while loaded_steps < min(coming + LOAD_LEAD, STEPS):
+                load(loaded_steps)
+                loaded_steps += 1
+            due = 2 * B * now + B - chores_done
+            if tick > 0 and chores and chores[0][0] <= coming:
+                due = max(due, 1)
+            chores_done += do_chores(due)
+            if tick == POWERS_TICK:
+                build_powers(1)
+            if tick == MASKS_TICK:
                 build_masks(1)
             if tick < len(order):
                 index = order[tick]
-                matrix, factor = mask_of(*banks[index])
+                bank = banks[index]
+                head = bank["step"] // CHUNKS
                 if by_scalar(index):
                     scalar_bank = psum_scalar.tile([P, PACK, P], F32, name="scalar_bank")
-                    products(scalar_bank, *banks[index])
+                    products(scalar_bank, bank)
                     moved = moved_pool.tile([P, P, PACK], F32)
                     nc.scalar.activation(
                         out=moved[:],
                         in_=scalar_bank[:].rearrange("p t w -> p w t"),
                         func=mybir.ActivationFunctionType.Copy,
-                        scale=factor,
+                        scale=GAMMA[head] ** bank["power"],
                     )
                     nc.gpsimd.tensor_tensor(
                         out=place_of(index),
                         in0=moved[:],
-                        in1=matrix[:],
+                        in1=bank["masks"][(head, bank["key"])][:],
                         op=mybir.AluOpType.mult,
                     )
                 else:
                     sim_ps = psum_sim.tile([P, PACK, P], F32)
-                    products(sim_ps, *banks[index])
+                    products(sim_ps, bank)
                     vector_banks[index] = sim_ps
             if tick < AHEAD:
                 continue
             index = order[tick - AHEAD]
             if by_scalar(index):
                 continue
-            matrix, factor = mask_of(*banks[index])
+            bank = banks[index]
+            head = bank["step"] // CHUNKS
             nc.vector.scalar_tensor_tensor(
                 out=place_of(index),
                 in0=vector_banks[index][:].rearrange("p t w -> p w t"),
-                scalar=factor,
-                in1=matrix[:],
+                scalar=GAMMA[head] ** bank["power"],
+                in1=bank["masks"][(head, bank["key"])][:],
                 op0=mybir.AluOpType.mult,
                 op1=mybir.AluOpType.mult,
             )
@@ -283,11 +454,12 @@ def tile_multiscaleretention_pb_t_kernel(tc, q_rot, k_scaled, v, out):
             if index % GROUP == 0 and group > 0:
                 quantise(group_tiles[group - 1], banks[index - GROUP : index])
             else:
-                contract(PASSES_PER_TICK)
-            if index % GROUP == 1:
-                pair, chunk, slot, key_chunk = banks[group * GROUP + GROUP - 1]
-                while quantised_steps <= pair * CHUNKS + chunk:
-                    quantise_values(quantised_steps // CHUNKS, quantised_steps % CHUNKS)
-                    quantised_steps += 1
+                contract(PASSES_PER_TICK, tick)
+                coming = banks[min((group + 2) * GROUP, len(banks)) - 1]["step"]
+                if index >= FIRST_VALUES and quantised_halves < B * (coming + 1):
+                    due = 2 * B * (quantised_halves // B) + B + quantised_halves % B + 1 - chores_done
+                    chores_done += do_chores(due)
+                    quantise_values(quantised_halves % B, quantised_halves // B)
+                    quantised_halves += 1
         quantise(group_tiles[groups - 1], banks[len(banks) - GROUP :])
-        contract(len(pending))
+        contract(len(pending), len(order) + AHEAD + EMPTYING)

@@ -362,15 +362,12 @@ def tile_multiscaleretention_pb_t_kernel(tc, q_rot, k_scaled, v, out):
 
         order = []
         for group in range(groups):
-            own = [i for i in range(group * GROUP, (group + 1) * GROUP) if not by_scalar(i)]
-            early = range((group + 1) * GROUP, min((group + 2) * GROUP, len(banks)))
-            early = [i for i in early if by_scalar(i)]
-            split = len(own) - len(early) + 1
-            order.extend(own[:split])
-            for index, follower in zip(early, own[split:] + [None]):
-                order.append(index)
-                if follower is not None:
-                    order.append(follower)
+            for place in range(GROUP):
+                index = group * GROUP + place
+                if not by_scalar(index):
+                    order.append(index)
+                if index + GROUP < len(banks) and by_scalar(index + GROUP):
+                    order.append(index + GROUP)
 
         group_tiles = {}
 

@@ -32,7 +32,7 @@ SETS = 3
 LOAD_LEAD = 2
 PASSES_PER_TICK = 3
 POWERS_TICK, MASKS_TICK = 24, 30
-SCALAR_PLACES = (2, 5)
+SCALAR_PLACES = ()
 
 PAD = P - QUAD
 WORDS = D + D // 4
@@ -187,27 +187,20 @@ def tile_multiscaleretention_pb_t_kernel(tc, q_rot, k_scaled, v, out):
         build_powers(0)
         build_masks(0)
 
-        turned = {}
-
-        def border(step):
-            for batch in range(B):
-                kq = consts.tile([P, 2 * PACK, PAD + P], BF16, name="turned_%d_%d" % (batch, step))
-                zeros = slice(P, PAD + P) if batch == 0 else slice(0, PAD)
-                nc.gpsimd.memset(kq[:, 0:PACK, zeros], 0.0)
-                turned[(batch, step)] = kq
-
-        for step in range(LOAD_LEAD):
-            border(step)
+        turned = []
+        for step in range(STEPS):
+            kq = consts.tile([P, 2 * PACK, P + PAD + P], BF16, name="turned_%d" % step)
+            nc.vector.memset(kq[:, 0:PACK, P : P + PAD], 0.0)
+            turned.append(kq)
+        own_columns = (slice(0, P), slice(P + PAD, P + PAD + P))
 
         moved_values = []
         for number in range(SETS):
             value_set = consts.tile(
                 [P, B, LAST, WORDS], U32, name="moved_values_%d" % number, align_bytes=64
             )
-            nc.gpsimd.memset(value_set[:], 0)
+            nc.vector.memset(value_set[:], 0)
             moved_values.append(value_set)
-        for step in range(LOAD_LEAD, STEPS):
-            border(step)
 
         v_grouped = {}
         v_quantised = {}
@@ -222,9 +215,7 @@ def tile_multiscaleretention_pb_t_kernel(tc, q_rot, k_scaled, v, out):
                 nc.tensor.transpose(
                     turned_ps[:, PACK + t, :], rows[("q", batch, step)][:, t, :], identity[:]
                 )
-            kq = turned[(batch, step)]
-            data = slice(0, P) if batch == 0 else slice(PAD, PAD + P)
-            nc.scalar.copy(out=kq[:, :, data], in_=turned_ps[:])
+            nc.scalar.copy(out=turned[step][:, :, own_columns[batch]], in_=turned_ps[:])
 
         def interleave(batch, step):
             values = interleaved.tile([P, D, PACK], BF16, align_bytes=64)
@@ -256,12 +247,11 @@ def tile_multiscaleretention_pb_t_kernel(tc, q_rot, k_scaled, v, out):
             for t in range(PACK):
                 for number, (batch, step, slot, key_step) in enumerate(bank["parts"]):
                     tiles = QUADS if key_step < step else slot + 1
-                    start = P - QUAD * tiles if batch == 0 else QUAD * tiles - (P - PAD)
-                    first = 0 if batch == 0 else PAD
+                    start = P - QUAD * tiles if batch == 0 else PAD + QUAD * tiles
                     nc.tensor.matmul(
                         out=bank_ps[:, t, :],
-                        lhsT=turned[(batch, key_step)][:, t, start : start + P],
-                        rhs=turned[(batch, step)][:, PACK + slot, first : first + P],
+                        lhsT=turned[key_step][:, t, start : start + P],
+                        rhs=turned[step][:, PACK + slot, own_columns[batch]],
                         start=(number == 0),
                         stop=(number == len(bank["parts"]) - 1),
                     )

@@ -32,7 +32,7 @@ SETS = 3
 LOAD_LEAD = 2
 PASSES_PER_TICK = 3
 POWERS_TICK, MASKS_TICK = 24, 30
-SCALAR_PLACES = ()
+SCALAR_PLACES = (2, 5)
 
 PAD = P - QUAD
 WORDS = D + D // 4
@@ -184,23 +184,29 @@ def tile_multiscaleretention_pb_t_kernel(tc, q_rot, k_scaled, v, out):
                     )
                 shared_masks[(head, tile_0)] = shared_mask
 
-        build_powers(0)
-        build_masks(0)
-
-        turned = []
-        for step in range(STEPS):
-            kq = consts.tile([P, 2 * PACK, P + PAD + P], BF16, name="turned_%d" % step)
-            nc.vector.memset(kq[:, 0:PACK, P : P + PAD], 0.0)
-            turned.append(kq)
+        turned = [
+            consts.tile([P, 2 * PACK, P + PAD + P], BF16, name="turned_%d" % step)
+            for step in range(STEPS)
+        ]
         own_columns = (slice(0, P), slice(P + PAD, P + PAD + P))
 
-        moved_values = []
+        moved_values = [
+            consts.tile([P, B, LAST, WORDS], U32, name="moved_values_%d" % number, align_bytes=64)
+            for number in range(SETS)
+        ]
+
+        zero_fills = [tile[:, 0:PACK, P : P + PAD] for tile in turned]
         for number in range(SETS):
-            value_set = consts.tile(
-                [P, B, LAST, WORDS], U32, name="moved_values_%d" % number, align_bytes=64
-            )
-            nc.vector.memset(value_set[:], 0)
-            moved_values.append(value_set)
+            zero_fills[2 * number + 2 : 2 * number + 2] = [moved_values[number][:]]
+
+        def zero_fill(count):
+            for region in zero_fills[:count]:
+                nc.vector.memset(region, 0)
+            zero_fills[:count] = []
+
+        zero_fill(3)
+        build_powers(0)
+        build_masks(0)
 
         v_grouped = {}
         v_quantised = {}
@@ -394,6 +400,8 @@ def tile_multiscaleretention_pb_t_kernel(tc, q_rot, k_scaled, v, out):
             if tick > 0 and chores and chores[0][0] <= coming:
                 due = max(due, 1)
             chores_done += do_chores(due)
+            if tick > AHEAD:
+                zero_fill(1)
             if tick == POWERS_TICK:
                 build_powers(1)
             if tick == MASKS_TICK:

@@ -19,21 +19,25 @@ CHUNK = P * PACK
 B, H, N, D = 2, 2, 2048, 128
 CHUNKS = N // CHUNK
 STEPS = H * CHUNKS
+LOAD_ORDER = (1, 0)
 LAST = QUADS - 1
 
 GAMMA = (1.0 - math.exp(math.log(2.0**-5)), 1.0 - math.exp(math.log(2.0**-9)))
 
+LAST_GROUPS = (4, 2, 2)
 GROUP = 8
 AHEAD = 3
 FIRST_VALUES = 3
 EMPTYING = 3
-CHORE_LEAD = 16
+TURN_LEAD, TURN_PACE = 40, 3
+INTERLEAVE_LEAD, INTERLEAVE_PACE = 20, 2
+TURN_TICKS = 3
 SETS = 3
 LOAD_LEAD = 2
 PASSES_PER_TICK = 3
 POWERS_TICK, MASKS_TICK = 24, 30
-SCALAR_PLACES = (2, 5)
-
+LONG_CHUNK = 2
+BY_SCALAR = 2
 PAD = P - QUAD
 WORDS = D + D // 4
 
@@ -62,7 +66,7 @@ def tile_multiscaleretention_pb_t_kernel(tc, q_rot, k_scaled, v, out):
         consts = ctx.enter_context(tc.tile_pool(name="consts", bufs=1))
         inputs = ctx.enter_context(tc.tile_pool(name="inputs", bufs=1))
         values_pool = ctx.enter_context(tc.tile_pool(name="values", bufs=2))
-        interleaved = ctx.enter_context(tc.tile_pool(name="interleaved", bufs=6))
+        interleaved = ctx.enter_context(tc.tile_pool(name="interleaved", bufs=8))
         work = ctx.enter_context(tc.tile_pool(name="work", bufs=3))
         grouped_pool = ctx.enter_context(tc.tile_pool(name="grouped", bufs=3))
         moved_pool = ctx.enter_context(tc.tile_pool(name="moved", bufs=3))
@@ -75,31 +79,32 @@ def tile_multiscaleretention_pb_t_kernel(tc, q_rot, k_scaled, v, out):
 
         def load(step):
             head, chunk = divmod(step, CHUNKS)
-            for which in ("k", "q", "v"):
-                for batch in range(B):
-                    first_row = (batch * H + head) * N + chunk * CHUNK
-                    loaded = inputs.tile(
-                        [P, PACK, D], BF16, name="%s_rows_%d_%d" % (which, batch, step)
+            loads = [(which, batch) for batch in LOAD_ORDER for which in ("k", "q")]
+            loads.extend(("v", batch) for batch in LOAD_ORDER)
+            for which, batch in loads:
+                first_row = (batch * H + head) * N + chunk * CHUNK
+                loaded = inputs.tile(
+                    [P, PACK, D], BF16, name="%s_rows_%d_%d" % (which, batch, step)
+                )
+                whole = flat_inputs[which][first_row : first_row + CHUNK, :]
+                if which == "q":
+                    nc.sync.dma_start(
+                        out=loaded[:], in_=whole.rearrange("(t p) d -> p t d", p=P)
                     )
-                    whole = flat_inputs[which][first_row : first_row + CHUNK, :]
-                    if which == "q":
+                elif batch == 1:
+                    nc.sync.dma_start(
+                        out=loaded[:], in_=whole.rearrange("(p t) d -> p t d", p=P)
+                    )
+                else:
+                    for quadrant in range(QUADS):
+                        first_key = P * (LAST - quadrant)
                         nc.sync.dma_start(
-                            out=loaded[:], in_=whole.rearrange("(t p) d -> p t d", p=P)
+                            out=loaded[QUAD * quadrant : QUAD * (quadrant + 1), :, :],
+                            in_=whole[first_key : first_key + P, :].rearrange(
+                                "(p t) d -> p t d", p=QUAD
+                            ),
                         )
-                    elif batch == 1:
-                        nc.sync.dma_start(
-                            out=loaded[:], in_=whole.rearrange("(p t) d -> p t d", p=P)
-                        )
-                    else:
-                        for quadrant in range(QUADS):
-                            first_key = P * (LAST - quadrant)
-                            nc.sync.dma_start(
-                                out=loaded[QUAD * quadrant : QUAD * (quadrant + 1), :, :],
-                                in_=whole[first_key : first_key + P, :].rearrange(
-                                    "(p t) d -> p t d", p=QUAD
-                                ),
-                            )
-                    rows[(which, batch, step)] = loaded
+                rows[(which, batch, step)] = loaded
 
         for step in range(LOAD_LEAD):
             load(step)
@@ -121,6 +126,25 @@ def tile_multiscaleretention_pb_t_kernel(tc, q_rot, k_scaled, v, out):
         )
         identity = consts.tile([P, P], BF16)
         make_identity(nc, identity[:])
+        identity_f32 = consts.tile([P, P], F32)
+        make_identity(nc, identity_f32[:])
+
+        query_part = consts.tile([P, PACK], F32)
+        nc.gpsimd.iota(
+            query_part[:],
+            pattern=[[-1, PACK]],
+            base=0,
+            channel_multiplier=1,
+            allow_small_or_imprecise_dtypes=True,
+        )
+        key_part = consts.tile([P, CHUNKS * PACK], F32)
+        nc.gpsimd.iota(
+            key_part[:],
+            pattern=[[P, CHUNKS * PACK]],
+            base=0,
+            channel_multiplier=-PACK,
+            allow_small_or_imprecise_dtypes=True,
+        )
 
         turned_back = consts.tile([P, 1], F32)
         for quadrant in range(QUADS):
@@ -145,6 +169,8 @@ def tile_multiscaleretention_pb_t_kernel(tc, q_rot, k_scaled, v, out):
 
         earlier_masks = {}
         last_masks = {}
+        query_factors = {}
+        key_factors = {}
         shared_masks = {}
 
         def build_powers(head):
@@ -159,7 +185,29 @@ def tile_multiscaleretention_pb_t_kernel(tc, q_rot, k_scaled, v, out):
                 )
                 earlier_masks[(head, batch)] = powers
 
-        def build_masks(head):
+        def build_factors(head):
+            factors = consts.tile([P, PACK], F32, name="query_factors_%d" % head)
+            nc.scalar.activation(
+                out=factors[:],
+                in_=query_part[:],
+                func=mybir.ActivationFunctionType.Exp,
+                scale=math.log(GAMMA[head]),
+            )
+            query_factors[head] = factors
+            for batch in range(B):
+                factors = consts.tile(
+                    [P, CHUNKS * PACK], F32, name="key_factors_%d_%d" % (head, batch)
+                )
+                nc.scalar.activation(
+                    out=factors[:],
+                    in_=key_part[:],
+                    func=mybir.ActivationFunctionType.Exp,
+                    bias=exponents[head][:] if batch == 0 else 0.0,
+                    scale=math.log(GAMMA[head]),
+                )
+                key_factors[(head, batch)] = factors
+
+        def build_last_masks(head):
             for batch in range(B):
                 last_mask = consts.tile([P, P, PACK], F32, name="last_%d_%d" % (head, batch))
                 nc.vector.scalar_tensor_tensor(
@@ -171,6 +219,8 @@ def tile_multiscaleretention_pb_t_kernel(tc, q_rot, k_scaled, v, out):
                     op1=mybir.AluOpType.mult,
                 )
                 last_masks[(head, batch)] = last_mask
+
+        def build_shared_masks(head):
             for tile_0 in SHARED_TILES:
                 shared_mask = consts.tile(
                     [P, P, PACK], F32, name="shared_%d_%d" % (head, tile_0)
@@ -178,10 +228,20 @@ def tile_multiscaleretention_pb_t_kernel(tc, q_rot, k_scaled, v, out):
                 for quadrants in SHARED_RUNS[tile_0]:
                     batch = 0 if quadrants.start <= tile_0 else 1
                     partitions = slice(QUAD * quadrants.start, QUAD * quadrants.stop)
-                    nc.vector.tensor_copy(
-                        out=shared_mask[partitions, :, :],
-                        in_=last_masks[(head, batch)][partitions, :, :],
-                    )
+                    if head == 0:
+                        nc.vector.tensor_copy(
+                            out=shared_mask[partitions, :, :],
+                            in_=last_masks[(head, batch)][partitions, :, :],
+                        )
+                    else:
+                        nc.gpsimd.tensor_scalar(
+                            out=shared_mask[partitions, :, :],
+                            in0=last_masks[(head, batch)][partitions, :, :],
+                            scalar1=1.0,
+                            scalar2=0.0,
+                            op0=mybir.AluOpType.mult,
+                            op1=mybir.AluOpType.add,
+                        )
                 shared_masks[(head, tile_0)] = shared_mask
 
         turned = [
@@ -206,7 +266,7 @@ def tile_multiscaleretention_pb_t_kernel(tc, q_rot, k_scaled, v, out):
 
         zero_fill(3)
         build_powers(0)
-        build_masks(0)
+        build_last_masks(0)
 
         v_grouped = {}
         v_quantised = {}
@@ -262,28 +322,65 @@ def tile_multiscaleretention_pb_t_kernel(tc, q_rot, k_scaled, v, out):
                         stop=(number == len(bank["parts"]) - 1),
                     )
 
-        def store(acc, batch, step):
+        def weight_queries(bank):
+            batch, step, slot, key_step = bank["parts"][0]
+            head = step // CHUNKS
+            sim_ps = psum_scalar.tile([P, PACK, P], F32, name="scalar_bank")
+            nc.tensor.matmul(
+                out=sim_ps[:],
+                lhsT=turned[step][:, PACK + slot, own_columns[batch]],
+                rhs=turned[key_step][:, 0:PACK, own_columns[batch]],
+                start=True,
+                stop=True,
+            )
+            half_done = moved_pool.tile([P, PACK, P], F32)
+            for t in range(PACK):
+                nc.scalar.activation(
+                    out=half_done[:, t, :],
+                    in_=sim_ps[:, t, :],
+                    func=mybir.ActivationFunctionType.Copy,
+                    scale=query_factors[head][:, t : t + 1],
+                )
+            return half_done
+
+        def weight_keys(half_done, bank, grouped_bank):
+            batch, step, slot, key_step = bank["parts"][0]
+            head = step // CHUNKS
+            tiles_on = PACK * (step - key_step) + slot
+            turned_ps = psum_scalar.tile([P, PACK, P], F32, name="scalar_bank")
+            for t in range(PACK):
+                nc.tensor.transpose(turned_ps[:, t, :], half_done[:, t, :], identity_f32[:])
+            nc.scalar.activation(
+                out=grouped_bank,
+                in_=turned_ps[:].rearrange("p t w -> p w t"),
+                func=mybir.ActivationFunctionType.Copy,
+                scale=key_factors[(head, batch)][:, tiles_on : tiles_on + 1],
+            )
+
+        def store(acc, batch, step, slots):
             head, chunk = divmod(step, CHUNKS)
             result = results.tile([P, QUADS, D], F32)
-            nc.scalar.copy(out=result[:], in_=acc[:])
+            nc.scalar.copy(out=result[:, slots, :], in_=acc[:, slots, :])
             first_row = batch * N + chunk * CHUNK
             nc.scalar.dma_start(
                 out=out_flat[
-                    first_row : first_row + CHUNK, head * D : (head + 1) * D
+                    first_row + P * slots.start : first_row + P * slots.stop,
+                    head * D : (head + 1) * D,
                 ].rearrange("(t p) d -> p t d", p=P),
-                in_=result[:],
+                in_=result[:, slots, :],
             )
 
         accs = {}
         pending = []
 
         def quantise(grouped, members):
+            count = len(members)
             codes = work.tile([P, GROUP, P], U32, align_bytes=64)
             scales = work.tile([P, GROUP, P], U8, align_bytes=64)
             nc.vector.quantize_mx(
-                out=codes[:].rearrange("p b w -> p (b w)").bitcast(FP8X4),
-                scales=scales[:].rearrange("p b w -> p (b w)"),
-                in_=grouped[:].rearrange("p b w t -> p (b w t)"),
+                out=codes[:, 0:count, :].rearrange("p b w -> p (b w)").bitcast(FP8X4),
+                scales=scales[:, 0:count, :].rearrange("p b w -> p (b w)"),
+                in_=grouped[:, 0:count, :, :].rearrange("p b w t -> p (b w t)"),
             )
             for place, bank in enumerate(members):
                 for part in bank["parts"]:
@@ -317,8 +414,12 @@ def tile_multiscaleretention_pb_t_kernel(tc, q_rot, k_scaled, v, out):
                 )
                 if key_step == step:
                     passes_left[(batch, step)] -= 1
+                    last_step = step == STEPS - 1
+                    if last_step and passes_left[(batch, step)] == 1:
+                        store(accs[(batch, step)], batch, step, slice(0, LAST))
                     if passes_left[(batch, step)] == 0:
-                        store(accs[(batch, step)], batch, step)
+                        slots = slice(LAST if last_step else 0, QUADS)
+                        store(accs[(batch, step)], batch, step, slots)
                         stored_at[batch] = tick
                 issued += 1
             pending[:] = pending[issued:]
@@ -341,102 +442,120 @@ def tile_multiscaleretention_pb_t_kernel(tc, q_rot, k_scaled, v, out):
                 power = CHUNK * (step - key_step) + P * slot
                 add(step, earlier_masks, batch, power, [(batch, step, slot, key_step)])
 
+        def add_last_tiles(step):
+            for batch in LOAD_ORDER if step == 0 else range(B):
+                add_earlier(batch, step, LAST)
+                add(step, last_masks, batch, P * LAST, [(batch, step, LAST, step)])
+
         for step in range(STEPS):
+            if step == 0:
+                add_last_tiles(step)
             for tile_0 in SHARED_TILES:
                 tile_1 = LAST - 1 - tile_0
                 add_earlier(0, step, tile_0)
                 add_earlier(1, step, tile_1)
                 parts = [(0, step, tile_0, step), (1, step, tile_1, step)]
                 add(step, shared_masks, tile_0, P * LAST, parts)
-            for batch in range(B):
-                add_earlier(batch, step, LAST)
-                add(step, last_masks, batch, P * LAST, [(batch, step, LAST, step)])
-        groups = len(banks) // GROUP
+            if step > 0:
+                add_last_tiles(step)
+        firsts = list(range(0, len(banks) - sum(LAST_GROUPS), GROUP))
+        for number in range(len(LAST_GROUPS)):
+            firsts.append(len(banks) - sum(LAST_GROUPS[number:]))
+        groups = len(firsts)
+        firsts.append(len(banks))
+        group_of = [g for g in range(groups) for i in range(firsts[g], firsts[g + 1])]
 
-        def by_scalar(index):
-            return index >= GROUP and index % GROUP in SCALAR_PLACES
+        by_scalar = []
+        for group in range(groups):
+            own = range(firsts[group] + 1, firsts[group + 1])
+            full = [
+                index
+                for index in own
+                if banks[index]["masks"] is earlier_masks
+                and banks[index]["step"] % CHUNKS >= LONG_CHUNK
+            ]
+            whole = 0 < group < groups - len(LAST_GROUPS)
+            by_scalar.append(full[max(len(full) - BY_SCALAR, 0) :] if whole else [])
 
         order = []
         for group in range(groups):
-            for place in range(GROUP):
-                index = group * GROUP + place
-                if not by_scalar(index):
-                    order.append(index)
-                if index + GROUP < len(banks) and by_scalar(index + GROUP):
-                    order.append(index + GROUP)
+            own = [
+                (index, "vector")
+                for index in range(firsts[group], firsts[group + 1])
+                if index not in by_scalar[group]
+            ]
+            for number, index in enumerate(by_scalar[group + 1] if group + 1 < groups else []):
+                own.insert(1 + number * (TURN_TICKS + 1), (index, "queries"))
+                own.insert(1 + number * (TURN_TICKS + 1) + TURN_TICKS, (index, "keys"))
+            order.extend(own)
 
         group_tiles = {}
 
         def place_of(index):
-            group = index // GROUP
+            group = group_of[index]
             if group not in group_tiles:
                 grouped = grouped_pool.tile([P, GROUP, P, PACK], BF16, align_bytes=64)
                 group_tiles[group] = grouped
-            return group_tiles[group][:, index % GROUP, :, :]
+            return group_tiles[group][:, index - firsts[group], :, :]
 
         loaded_steps = LOAD_LEAD
-        chores = []
-        for step in range(STEPS):
-            chores.extend((step, turn, batch) for batch in range(B))
-            chores.extend((step, interleave, batch) for batch in range(B))
-        chores_done = 0
+        turns = [(step, batch) for step in range(STEPS) for batch in LOAD_ORDER]
+        interleaves = list(turns)
 
-        def do_chores(due):
-            done = max(due, 0)
-            for step, chore, batch in chores[:done]:
+        def do_chores(chore, queue, due, coming):
+            if due <= 0 and queue and queue[0][0] <= coming:
+                due = 1
+            for step, batch in queue[: max(due, 0)]:
                 chore(batch, step)
-            chores[:done] = []
-            return done
+            queue[:] = queue[max(due, 0) :]
+
+        def step_at(place):
+            return banks[order[min(place, len(order) - 1)][0]]["step"]
 
         quantised_halves = 0
         vector_banks = {}
+        weighted = {}
         for tick in range(len(order) + AHEAD):
-            now = banks[order[min(tick, len(order) - 1)]]["step"]
-            coming = banks[order[min(tick + CHORE_LEAD, len(order) - 1)]]["step"]
+            coming = step_at(tick + TURN_LEAD)
             while loaded_steps < min(coming + LOAD_LEAD, STEPS):
                 load(loaded_steps)
                 loaded_steps += 1
-            due = 2 * B * now + B - chores_done
-            if tick > 0 and chores and chores[0][0] <= coming:
-                due = max(due, 1)
-            chores_done += do_chores(due)
+            needed = B * step_at(tick) + (1 if tick == 0 else B)
+            due = needed - (B * STEPS - len(turns))
+            do_chores(turn, turns, due, coming if tick % TURN_PACE == TURN_PACE - 1 else -1)
+            if tick % INTERLEAVE_PACE == INTERLEAVE_PACE - 1:
+                do_chores(interleave, interleaves, 0, step_at(tick + INTERLEAVE_LEAD))
             if tick > AHEAD:
                 zero_fill(1)
+            if tick == 1:
+                build_factors(0)
             if tick == POWERS_TICK:
                 build_powers(1)
+                build_factors(1)
             if tick == MASKS_TICK:
-                build_masks(1)
+                build_last_masks(1)
+                build_shared_masks(1)
             if tick < len(order):
-                index = order[tick]
+                index, half = order[tick]
                 bank = banks[index]
                 head = bank["step"] // CHUNKS
-                if by_scalar(index):
-                    scalar_bank = psum_scalar.tile([P, PACK, P], F32, name="scalar_bank")
-                    products(scalar_bank, bank)
-                    moved = moved_pool.tile([P, P, PACK], F32)
-                    nc.scalar.activation(
-                        out=moved[:],
-                        in_=scalar_bank[:].rearrange("p t w -> p w t"),
-                        func=mybir.ActivationFunctionType.Copy,
-                        scale=GAMMA[head] ** bank["power"],
-                    )
-                    nc.gpsimd.tensor_tensor(
-                        out=place_of(index),
-                        in0=moved[:],
-                        in1=bank["masks"][(head, bank["key"])][:],
-                        op=mybir.AluOpType.mult,
-                    )
+                if half == "queries":
+                    weighted[index] = weight_queries(bank)
+                elif half == "keys":
+                    weight_keys(weighted[index], bank, place_of(index))
                 else:
                     sim_ps = psum_sim.tile([P, PACK, P], F32)
                     products(sim_ps, bank)
                     vector_banks[index] = sim_ps
             if tick < AHEAD:
                 continue
-            index = order[tick - AHEAD]
-            if by_scalar(index):
+            index, half = order[tick - AHEAD]
+            if half != "vector":
                 continue
             bank = banks[index]
             head = bank["step"] // CHUNKS
+            if (head, bank["key"]) not in bank["masks"]:
+                build_shared_masks(head)
             nc.vector.scalar_tensor_tensor(
                 out=place_of(index),
                 in0=vector_banks[index][:].rearrange("p t w -> p w t"),
@@ -445,16 +564,16 @@ def tile_multiscaleretention_pb_t_kernel(tc, q_rot, k_scaled, v, out):
                 op0=mybir.AluOpType.mult,
                 op1=mybir.AluOpType.mult,
             )
-            group = index // GROUP
-            if index % GROUP == 0 and group > 0:
-                quantise(group_tiles[group - 1], banks[index - GROUP : index])
+            group = group_of[index]
+            if index == firsts[group] and group > 0:
+                quantise(group_tiles[group - 1], banks[firsts[group - 1] : index])
             else:
                 contract(PASSES_PER_TICK, tick)
-                coming = banks[min((group + 2) * GROUP, len(banks)) - 1]["step"]
+                coming = banks[firsts[min(group + 2, groups)] - 1]["step"]
                 if index >= FIRST_VALUES and quantised_halves < B * (coming + 1):
-                    due = 2 * B * (quantised_halves // B) + B + quantised_halves % B + 1 - chores_done
-                    chores_done += do_chores(due)
-                    quantise_values(quantised_halves % B, quantised_halves // B)
+                    due = quantised_halves + 1 - (B * STEPS - len(interleaves))
+                    do_chores(interleave, interleaves, due, -1)
+                    quantise_values(LOAD_ORDER[quantised_halves % B], quantised_halves // B)
                     quantised_halves += 1
-        quantise(group_tiles[groups - 1], banks[len(banks) - GROUP :])
+        quantise(group_tiles[groups - 1], banks[firsts[groups - 1] :])
         contract(len(pending), len(order) + AHEAD + EMPTYING)

import math
from contextlib import ExitStack

import concourse.mybir as mybir
from concourse.masks import make_identity

BF16 = mybir.dt.bfloat16
F32 = mybir.dt.float32
I32 = mybir.dt.int32
U32 = mybir.dt.uint32
U8 = mybir.dt.uint8
FP8X4 = mybir.dt.float8_e4m3fn_x4

P = 128
PACK = 4
QUADS = 4
QUAD = P // QUADS
CHUNK = P * PACK
B, H, N, D = 2, 2, 2048, 128
CHUNKS = N // CHUNK
STEPS = H * CHUNKS
LOAD_ORDER = (1, 0)
LAST = QUADS - 1

GAMMA = (1.0 - math.exp(math.log(2.0**-5)), 1.0 - math.exp(math.log(2.0**-9)))

LAST_GROUPS = (4, 2, 2)
GROUP = 8
AHEAD = 3
FIRST_VALUES = 3
EMPTYING = 3
TURN_LEAD, TURN_PACE = 40, 3
INTERLEAVE_LEAD, INTERLEAVE_PACE = 20, 2
TURN_TICKS = 3
SETS = 3
LOAD_LEAD = 2
PASSES_PER_TICK = 3
POWERS_TICK, MASKS_TICK = 24, 30
LONG_CHUNK = 2
BY_SCALAR = 2
PAD = P - QUAD
WORDS = D + D // 4

FLOPS = 2 * 2 * D * B * H * CHUNK * CHUNK * (CHUNKS * (CHUNKS + 1) // 2)

SHARED_TILES = (2, 0, 1)

SHARED_RUNS = {
    0: (slice(0, 1), slice(1, 2), slice(2, 4)),
    1: (slice(0, 2), slice(2, 4)),
    2: (slice(0, 3), slice(3, 4)),
}


def tile_multiscaleretention_pb_t_kernel(tc, q_rot, k_scaled, v, out):
    nc = tc.nc
    flat_inputs = {
        "k": k_scaled.flatten_outer_dims(),
        "q": q_rot.flatten_outer_dims(),
        "v": v.flatten_outer_dims(),
    }
    out_flat = out.flatten_outer_dims()

    with ExitStack() as ctx:
        ctx.enter_context(tc.manual_schedule())
        consts = ctx.enter_context(tc.tile_pool(name="consts", bufs=1))
        inputs = ctx.enter_context(tc.tile_pool(name="inputs", bufs=1))
        values_pool = ctx.enter_context(tc.tile_pool(name="values", bufs=2))
        interleaved = ctx.enter_context(tc.tile_pool(name="interleaved", bufs=8))
        work = ctx.enter_context(tc.tile_pool(name="work", bufs=3))
        grouped_pool = ctx.enter_context(tc.tile_pool(name="grouped", bufs=3))
        moved_pool = ctx.enter_context(tc.tile_pool(name="moved", bufs=3))
        results = ctx.enter_context(tc.tile_pool(name="results", bufs=3))
        psum_scalar = ctx.enter_context(tc.psum_pool(name="psum_scalar", bufs=2))
        psum_sim = ctx.enter_context(tc.psum_pool(name="psum_sim", bufs=AHEAD + 1))
        psum_acc = ctx.enter_context(tc.psum_pool(name="psum_acc", bufs=1))

        rows = {}

        def load(step):
            head, chunk = divmod(step, CHUNKS)
            loads = [(which, batch) for batch in LOAD_ORDER for which in ("k", "q")]
            loads.extend(("v", batch) for batch in LOAD_ORDER)
            for which, batch in loads:
                first_row = (batch * H + head) * N + chunk * CHUNK
                loaded = inputs.tile(
                    [P, PACK, D], BF16, name="%s_rows_%d_%d" % (which, batch, step)
                )
                whole = flat_inputs[which][first_row : first_row + CHUNK, :]
                if which == "q":
                    nc.sync.dma_start(
                        out=loaded[:], in_=whole.rearrange("(t p) d -> p t d", p=P)
                    )
                elif batch == 1:
                    nc.sync.dma_start(
                        out=loaded[:], in_=whole.rearrange("(p t) d -> p t d", p=P)
                    )
                else:
                    for quadrant in range(QUADS):
                        first_key = P * (LAST - quadrant)
                        nc.sync.dma_start(
                            out=loaded[QUAD * quadrant : QUAD * (quadrant + 1), :, :],
                            in_=whole[first_key : first_key + P, :].rearrange(
                                "(p t) d -> p t d", p=QUAD
                            ),
                        )
                rows[(which, batch, step)] = loaded

        for step in range(LOAD_LEAD):
            load(step)

        warm = consts.tile([P, 1], F32)
        nc.vector.memset(warm[:], 0.0)
        warmed = consts.tile([P, 1], F32)
        nc.scalar.activation(
            out=warmed[:], in_=warm[:], func=mybir.ActivationFunctionType.Exp
        )

        distance = consts.tile([P, P, PACK], F32)
        nc.gpsimd.iota(
            distance[:],
            pattern=[[1, P], [-1, PACK]],
            base=0,
            channel_multiplier=-PACK,
            allow_small_or_imprecise_dtypes=True,
        )
        identity = consts.tile([P, P], BF16)
        make_identity(nc, identity[:])
        identity_f32 = consts.tile([P, P], F32)
        make_identity(nc, identity_f32[:])

        query_part = consts.tile([P, PACK], F32)
        nc.gpsimd.iota(
            query_part[:],
            pattern=[[-1, PACK]],
            base=0,
            channel_multiplier=1,
            allow_small_or_imprecise_dtypes=True,
        )
        key_part = consts.tile([P, CHUNKS * PACK], F32)
        nc.gpsimd.iota(
            key_part[:],
            pattern=[[P, CHUNKS * PACK]],
            base=0,
            channel_multiplier=-PACK,
            allow_small_or_imprecise_dtypes=True,
        )

        turned_back = consts.tile([P, 1], F32)
        for quadrant in range(QUADS):
            nc.vector.memset(
                turned_back[QUAD * quadrant : QUAD * (quadrant + 1), :],
                float(2 * P * quadrant),
            )
        first_causal = consts.tile([P, 1], F32)
        nc.vector.tensor_scalar_mul(out=first_causal[:], in0=turned_back[:], scalar1=-1.0)
        exponents = []
        for head in range(H):
            head_exponents = consts.tile([P, 1], F32, name="exponents_%d" % head)
            nc.vector.tensor_scalar(
                out=head_exponents[:],
                in0=turned_back[:],
                scalar1=float(-P * LAST),
                scalar2=math.log(GAMMA[head]),
                op0=mybir.AluOpType.add,
                op1=mybir.AluOpType.mult,
            )
            exponents.append(head_exponents)

        earlier_masks = {}
        last_masks = {}
        query_factors = {}
        key_factors = {}
        shared_masks = {}

        def build_powers(head):
            for batch in range(B):
                powers = consts.tile([P, P, PACK], F32, name="powers_%d_%d" % (head, batch))
                nc.scalar.activation(
                    out=powers[:],
                    in_=distance[:],
                    func=mybir.ActivationFunctionType.Exp,
                    bias=exponents[head][:] if batch == 0 else 0.0,
                    scale=math.log(GAMMA[head]),
                )
                earlier_masks[(head, batch)] = powers

        def build_factors(head):
            factors = consts.tile([P, PACK], F32, name="query_factors_%d" % head)
            nc.scalar.activation(
                out=factors[:],
                in_=query_part[:],
                func=mybir.ActivationFunctionType.Exp,
                scale=math.log(GAMMA[head]),
            )
            query_factors[head] = factors
            for batch in range(B):
                factors = consts.tile(
                    [P, CHUNKS * PACK], F32, name="key_factors_%d_%d" % (head, batch)
                )
                nc.scalar.activation(
                    out=factors[:],
                    in_=key_part[:],
                    func=mybir.ActivationFunctionType.Exp,
                    bias=exponents[head][:] if batch == 0 else 0.0,
                    scale=math.log(GAMMA[head]),
                )
                key_factors[(head, batch)] = factors

        def build_last_masks(head):
            for batch in range(B):
                last_mask = consts.tile([P, P, PACK], F32, name="last_%d_%d" % (head, batch))
                nc.vector.scalar_tensor_tensor(
                    out=last_mask[:],
                    in0=distance[:],
                    scalar=first_causal[:] if batch == 0 else float(-P * LAST),
                    in1=earlier_masks[(head, batch)][:],
                    op0=mybir.AluOpType.is_ge,
                    op1=mybir.AluOpType.mult,
                )
                last_masks[(head, batch)] = last_mask

        def build_shared_masks(head):
            for tile_0 in SHARED_TILES:
                shared_mask = consts.tile(
                    [P, P, PACK], F32, name="shared_%d_%d" % (head, tile_0)
                )
                for quadrants in SHARED_RUNS[tile_0]:
                    batch = 0 if quadrants.start <= tile_0 else 1
                    partitions = slice(QUAD * quadrants.start, QUAD * quadrants.stop)
                    if head == 0:
                        nc.vector.tensor_copy(
                            out=shared_mask[partitions, :, :],
                            in_=last_masks[(head, batch)][partitions, :, :],
                        )
                    else:
                        nc.gpsimd.tensor_scalar(
                            out=shared_mask[partitions, :, :],
                            in0=last_masks[(head, batch)][partitions, :, :],
                            scalar1=1.0,
                            scalar2=0.0,
                            op0=mybir.AluOpType.mult,
                            op1=mybir.AluOpType.add,
                        )
                shared_masks[(head, tile_0)] = shared_mask

        turned = [
            consts.tile([P, 2 * PACK, P + PAD + P], BF16, name="turned_%d" % step)
            for step in range(STEPS)
        ]
        own_columns = (slice(0, P), slice(P + PAD, P + PAD + P))

        moved_values = [
            consts.tile([P, B, LAST, WORDS], U32, name="moved_values_%d" % number, align_bytes=64)
            for number in range(SETS)
        ]

        zero_fills = [tile[:, 0:PACK, P : P + PAD] for tile in turned]
        for number in range(SETS):
            zero_fills[2 * number + 2 : 2 * number + 2] = [moved_values[number][:]]

        def zero_fill(count):
            for region in zero_fills[:count]:
                nc.vector.memset(region, 0)
            zero_fills[:count] = []

        zero_fill(3)
        build_powers(0)
        build_last_masks(0)

        v_grouped = {}
        v_quantised = {}

        def turn(batch, step):
            turned_ps = psum_scalar.tile([P, 2 * PACK, P], BF16, name="scalar_bank")
            for t in range(PACK):
                nc.tensor.transpose(
                    turned_ps[:, t, :], rows[("k", batch, step)][:, t, :], identity[:]
                )
            for t in range(PACK):
                nc.tensor.transpose(
                    turned_ps[:, PACK + t, :], rows[("q", batch, step)][:, t, :], identity[:]
                )
            nc.scalar.copy(out=turned[step][:, :, own_columns[batch]], in_=turned_ps[:])

        def interleave(batch, step):
            values = interleaved.tile([P, D, PACK], BF16, align_bytes=64)
            nc.scalar.copy(
                out=values[:], in_=rows[("v", batch, step)][:].rearrange("p t d -> p d t")
            )
            v_grouped[(batch, step)] = values

        def quantise_values(batch, step):
            words = values_pool.tile(
                [P, WORDS], U32, name="values_%d_%d" % (batch, step % CHUNKS), align_bytes=64
            )
            nc.vector.quantize_mx(
                out=words[:, 0:D].bitcast(FP8X4),
                scales=words[:, D:WORDS].bitcast(U8),
                in_=v_grouped[(batch, step)][:].rearrange("p d t -> p (d t)"),
            )
            v_quantised[(batch, step)] = words
            for tiles in range(1, QUADS):
                far_end = slice(P - QUAD * tiles, P)
                near_end = slice(0, QUAD * tiles)
                source, target = (far_end, near_end) if batch == 0 else (near_end, far_end)
                nc.sync.dma_start(
                    out=moved_values[step % SETS][target, batch, tiles - 1, :].bitcast(I32),
                    in_=words[source, :].bitcast(I32),
                )

        def products(bank_ps, bank):
            for t in range(PACK):
                for number, (batch, step, slot, key_step) in enumerate(bank["parts"]):
                    tiles = QUADS if key_step < step else slot + 1
                    start = P - QUAD * tiles if batch == 0 else PAD + QUAD * tiles
                    nc.tensor.matmul(
                        out=bank_ps[:, t, :],
                        lhsT=turned[key_step][:, t, start : start + P],
                        rhs=turned[step][:, PACK + slot, own_columns[batch]],
                        start=(number == 0),
                        stop=(number == len(bank["parts"]) - 1),
                    )

        def weight_queries(bank):
            batch, step, slot, key_step = bank["parts"][0]
            head = step // CHUNKS
            sim_ps = psum_scalar.tile([P, PACK, P], F32, name="scalar_bank")
            nc.tensor.matmul(
                out=sim_ps[:],
                lhsT=turned[step][:, PACK + slot, own_columns[batch]],
                rhs=turned[key_step][:, 0:PACK, own_columns[batch]],
                start=True,
                stop=True,
            )
            half_done = moved_pool.tile([P, PACK, P], F32)
            for t in range(PACK):
                nc.scalar.activation(
                    out=half_done[:, t, :],
                    in_=sim_ps[:, t, :],
                    func=mybir.ActivationFunctionType.Copy,
                    scale=query_factors[head][:, t : t + 1],
                )
            return half_done

        def weight_keys(half_done, bank, grouped_bank):
            batch, step, slot, key_step = bank["parts"][0]
            head = step // CHUNKS
            tiles_on = PACK * (step - key_step) + slot
            turned_ps = psum_scalar.tile([P, PACK, P], F32, name="scalar_bank")
            for t in range(PACK):
                nc.tensor.transpose(turned_ps[:, t, :], half_done[:, t, :], identity_f32[:])
            nc.scalar.activation(
                out=grouped_bank,
                in_=turned_ps[:].rearrange("p t w -> p w t"),
                func=mybir.ActivationFunctionType.Copy,
                scale=key_factors[(head, batch)][:, tiles_on : tiles_on + 1],
            )

        def store(acc, batch, step, slots):
            head, chunk = divmod(step, CHUNKS)
            result = results.tile([P, QUADS, D], F32)
            nc.scalar.copy(out=result[:, slots, :], in_=acc[:, slots, :])
            first_row = batch * N + chunk * CHUNK
            nc.scalar.dma_start(
                out=out_flat[
                    first_row + P * slots.start : first_row + P * slots.stop,
                    head * D : (head + 1) * D,
                ].rearrange("(t p) d -> p t d", p=P),
                in_=result[:, slots, :],
            )

        accs = {}
        pending = []

        def quantise(grouped, members):
            count = len(members)
            codes = work.tile([P, GROUP, P], U32, align_bytes=64)
            scales = work.tile([P, GROUP, P], U8, align_bytes=64)
            nc.vector.quantize_mx(
                out=codes[:, 0:count, :].rearrange("p b w -> p (b w)").bitcast(FP8X4),
                scales=scales[:, 0:count, :].rearrange("p b w -> p (b w)"),
                in_=grouped[:, 0:count, :, :].rearrange("p b w t -> p (b w t)"),
            )
            for place, bank in enumerate(members):
                for part in bank["parts"]:
                    pending.append((codes[:, place, :], scales[:, place, :], part))

        passes_left = {}

        stored_at = {0: -EMPTYING, 1: -EMPTYING}

        def contract(count, tick):
            issued = 0
            for codes, scales, (batch, step, slot, key_step) in pending[:count]:
                if (batch, step) not in accs:
                    if tick < stored_at[batch] + EMPTYING:
                        break
                    acc = psum_acc.tile([P, QUADS, D], F32, name="acc_%d" % batch)
                    accs[(batch, step)] = acc
                    passes_left[(batch, step)] = QUADS
                if key_step < step or slot == LAST:
                    words = v_quantised[(batch, key_step)][:]
                else:
                    words = moved_values[step % SETS][:, batch, slot, :]
                nc.tensor.matmul_mx(
                    out=accs[(batch, step)][:, slot, :],
                    lhsT=codes.bitcast(FP8X4),
                    lhsT_scale=scales,
                    rhs=words[:, 0:D].bitcast(FP8X4),
                    rhs_scale=words[:, D:WORDS].bitcast(U8),
                    start=(key_step % CHUNKS == 0),
                    stop=(key_step == step),
                )
                if key_step == step:
                    passes_left[(batch, step)] -= 1
                    last_step = step == STEPS - 1
                    if last_step and passes_left[(batch, step)] == 1:
                        store(accs[(batch, step)], batch, step, slice(0, LAST))
                    if passes_left[(batch, step)] == 0:
                        slots = slice(LAST if last_step else 0, QUADS)
                        store(accs[(batch, step)], batch, step, slots)
                        stored_at[batch] = tick
                issued += 1
            pending[:] = pending[issued:]

        banks = []

        def add(step, masks, key, power, parts):
            banks.append(
                {
                    "step": step,
                    "masks": masks,
                    "key": key,
                    "power": power,
                    "parts": parts,
                }
            )

        def add_earlier(batch, step, slot):
            for key_step in range(step - step % CHUNKS, step):
                power = CHUNK * (step - key_step) + P * slot
                add(step, earlier_masks, batch, power, [(batch, step, slot, key_step)])

        def add_last_tiles(step):
            for batch in LOAD_ORDER if step == 0 else range(B):
                add_earlier(batch, step, LAST)
                add(step, last_masks, batch, P * LAST, [(batch, step, LAST, step)])

        for step in range(STEPS):
            if step == 0:
                add_last_tiles(step)
            for tile_0 in SHARED_TILES:
                tile_1 = LAST - 1 - tile_0
                add_earlier(0, step, tile_0)
                add_earlier(1, step, tile_1)
                parts = [(0, step, tile_0, step), (1, step, tile_1, step)]
                add(step, shared_masks, tile_0, P * LAST, parts)
            if step > 0:
                add_last_tiles(step)
        firsts = list(range(0, len(banks) - sum(LAST_GROUPS), GROUP))
        for number in range(len(LAST_GROUPS)):
            firsts.append(len(banks) - sum(LAST_GROUPS[number:]))
        groups = len(firsts)
        firsts.append(len(banks))
        group_of = [g for g in range(groups) for i in range(firsts[g], firsts[g + 1])]

        by_scalar = []
        for group in range(groups):
            own = range(firsts[group] + 1, firsts[group + 1])
            full = [
                index
                for index in own
                if banks[index]["masks"] is earlier_masks
                and banks[index]["step"] % CHUNKS >= LONG_CHUNK
            ]
            whole = 0 < group < groups - len(LAST_GROUPS)
            by_scalar.append(full[max(len(full) - BY_SCALAR, 0) :] if whole else [])

        order = []
        for group in range(groups):
            own = [
                (index, "vector")
                for index in range(firsts[group], firsts[group + 1])
                if index not in by_scalar[group]
            ]
            for number, index in enumerate(by_scalar[group + 1] if group + 1 < groups else []):
                own.insert(1 + number * (TURN_TICKS + 1), (index, "queries"))
                own.insert(1 + number * (TURN_TICKS + 1) + TURN_TICKS, (index, "keys"))
            order.extend(own)

        group_tiles = {}

        def place_of(index):
            group = group_of[index]
            if group not in group_tiles:
                grouped = grouped_pool.tile([P, GROUP, P, PACK], BF16, align_bytes=64)
                group_tiles[group] = grouped
            return group_tiles[group][:, index - firsts[group], :, :]

        loaded_steps = LOAD_LEAD
        turns = [(step, batch) for step in range(STEPS) for batch in LOAD_ORDER]
        interleaves = list(turns)

        def do_chores(chore, queue, due, coming):
            if due <= 0 and queue and queue[0][0] <= coming:
                due = 1
            for step, batch in queue[: max(due, 0)]:
                chore(batch, step)
            queue[:] = queue[max(due, 0) :]

        def step_at(place):
            return banks[order[min(place, len(order) - 1)][0]]["step"]

        quantised_halves = 0
        vector_banks = {}
        weighted = {}
        for tick in range(len(order) + AHEAD):
            coming = step_at(tick + TURN_LEAD)
            while loaded_steps < min(coming + LOAD_LEAD, STEPS):
                load(loaded_steps)
                loaded_steps += 1
            needed = B * step_at(tick) + (1 if tick == 0 else B)
            due = needed - (B * STEPS - len(turns))
            do_chores(turn, turns, due, coming if tick % TURN_PACE == TURN_PACE - 1 else -1)
            if tick % INTERLEAVE_PACE == INTERLEAVE_PACE - 1:
                do_chores(interleave, interleaves, 0, step_at(tick + INTERLEAVE_LEAD))
            if tick > AHEAD:
                zero_fill(1)
            if tick == 1:
                build_factors(0)
            if tick == POWERS_TICK:
                build_powers(1)
                build_factors(1)
            if tick == MASKS_TICK:
                build_last_masks(1)
                build_shared_masks(1)
            if tick < len(order):
                index, half = order[tick]
                bank = banks[index]
                head = bank["step"] // CHUNKS
                if half == "queries":
                    weighted[index] = weight_queries(bank)
                elif half == "keys":
                    weight_keys(weighted[index], bank, place_of(index))
                else:
                    sim_ps = psum_sim.tile([P, PACK, P], F32)
                    products(sim_ps, bank)
                    vector_banks[index] = sim_ps
            if tick < AHEAD:
                continue
            index, half = order[tick - AHEAD]
            if half != "vector":
                continue
            bank = banks[index]
            head = bank["step"] // CHUNKS
            if (head, bank["key"]) not in bank["masks"]:
                build_shared_masks(head)
            nc.vector.scalar_tensor_tensor(
                out=place_of(index),
                in0=vector_banks[index][:].rearrange("p t w -> p w t"),
                scalar=GAMMA[head] ** bank["power"],
                in1=bank["masks"][(head, bank["key"])][:],
                op0=mybir.AluOpType.mult,
                op1=mybir.AluOpType.mult,
            )
            group = group_of[index]
            if index == firsts[group] and group > 0:
                quantise(group_tiles[group - 1], banks[firsts[group - 1] : index])
            else:
                contract(PASSES_PER_TICK, tick)
                coming = banks[firsts[min(group + 2, groups)] - 1]["step"]
                if index >= FIRST_VALUES and quantised_halves < B * (coming + 1):
                    due = quantised_halves + 1 - (B * STEPS - len(interleaves))
                    do_chores(interleave, interleaves, due, -1)
                    quantise_values(LOAD_ORDER[quantised_halves % B], quantised_halves // B)
                    quantised_halves += 1
        quantise(group_tiles[groups - 1], banks[firsts[groups - 1] :])
        contract(len(pending), len(order) + AHEAD + EMPTYING)
